import numpy as np
import ml_dtypes


def mxq(x, axis, fmt="e4m3"):
    dtype, down = {"e4m3": (ml_dtypes.float8_e4m3fn, 7), "e5m2": (ml_dtypes.float8_e5m2, 14)}[fmt]
    v = np.moveaxis(np.asarray(x, np.float32).astype(ml_dtypes.bfloat16).astype(np.float64), axis, -1)
    blocks = v.reshape(v.shape[:-1] + (-1, 32))
    amax = np.abs(blocks).max(-1, keepdims=True)
    byte = np.maximum(np.where(amax > 0, np.frexp(amax)[1] - 1 + 127, 0) - down, 1)
    scale = np.exp2(byte - 127.0)
    codes = (blocks / scale).astype(np.float32).astype(dtype).astype(np.float64)
    return np.moveaxis((codes * scale).reshape(v.shape), -1, axis)


WIDE = False


def mx_kscale(k):
    if not WIDE:
        return np.ones(k)
    levels = np.array([10, -10, 5, -5, 0])
    a = np.random.permutation(np.resize(levels, k // 512 * 4)).reshape(k // 512, 4)
    idx = np.arange(k)
    return np.exp2(a[idx // 512, idx % 128 // 32])


BF16 = ml_dtypes.bfloat16


def bf(x):
    return np.asarray(x, np.float32).astype(BF16)


def f64(x):
    return np.asarray(x).astype(np.float64)


B, H, K = 4096, 512, 128
R = H ** -0.25


def setup_inputs():
    s = mx_kscale(H)
    return {
        "encoder_final_state": bf(np.random.standard_normal((B, H)) * s),
        "W_mu": bf(np.random.standard_normal((H, H)) * 0.55 * R / np.sqrt(H) / s[None, :]),
        "b_mu": bf(np.random.standard_normal(H) * 0.3 * R),
        "W_ls": bf(np.random.standard_normal((H, H)) * 0.5 / np.sqrt(H) / s[None, :]),
        "b_ls": bf(np.random.standard_normal(H) * 0.1),
        "mu_c": bf(np.random.standard_normal((K, H)) * 0.5 * R),
        "log_sigma_sq_c": bf(np.random.standard_normal((K, H)) * 0.4),
        "eps_z": bf(np.random.standard_normal((B, H)) * 0.55 * R),
    }


def reference(encoder_final_state, W_mu, b_mu, W_ls, b_ls, mu_c, log_sigma_sq_c, eps_z):
    xq = mxq(f64(encoder_final_state), 1, "e4m3")
    mu_z = (xq @ mxq(f64(W_mu), 1, "e4m3").T) + f64(b_mu)
    ls_z = (xq @ mxq(f64(W_ls), 1, "e4m3").T) + f64(b_ls)
    z = mu_z + np.exp(0.5 * ls_z) * f64(eps_z)
    inv_sig = np.exp(-f64(log_sigma_sq_c))
    mu_inv = f64(mu_c) * inv_sig
    c2 = np.sum(f64(mu_c) * mu_inv, axis=-1)
    d = (mxq(z * z, 1, "e4m3") @ mxq(inv_sig, 1, "e4m3").T) - 2.0 * (mxq(z, 1, "e4m3") @ mxq(mu_inv, 1, "e4m3").T) + c2[None, :]
    g = -d
    e = np.exp(g - g.max(-1, keepdims=True))
    att = e / e.sum(-1, keepdims=True)
    return z, att

@@ -1,0 +1,365 @@
+from contextlib import ExitStack
+
+import concourse.mybir as mybir
+from concourse.masks import make_identity
+
+F32 = mybir.dt.float32
+BF16 = mybir.dt.bfloat16
+U32 = mybir.dt.uint32
+U8 = mybir.dt.uint8
+FP8X4 = mybir.dt.float8_e4m3fn_x4
+ACT = mybir.ActivationFunctionType
+ALU = mybir.AluOpType
+
+P = 128
+PACK = 4
+B = 4096
+H = 512
+C = 128
+CHUNK = 512
+TILES = CHUNK // P
+H_TILES = H // P
+N_CHUNKS = B // CHUNK
+
+FILL_STEPS = 6
+DRAIN_STEPS = 8
+
+FLOPS = 2 * B * H * (2 * H) + 2 * B * H * (2 * C)
+
+
+def tile_latent_pa_t_kernel(
+    tc, encoder_final_state, W_mu, b_mu, W_ls, b_ls, mu_c, log_sigma_sq_c, eps_z, out_0, out_1
+):
+    nc = tc.nc
+
+    x_chunks = encoder_final_state.rearrange("(n p j) k -> n p (j k)", p=P, j=TILES)
+    eps_chunks = eps_z.rearrange("(n p j) h -> n p (j h)", p=P, j=TILES)
+    z_chunks = out_0.rearrange("(n p j) h -> n p (j h)", p=P, j=TILES)
+    att_chunks = out_1.rearrange("(n p j) c -> n p (j c)", p=P, j=TILES)
+
+    with ExitStack() as ctx:
+        ctx.enter_context(tc.manual_schedule())
+        const = ctx.enter_context(tc.tile_pool(name="const", bufs=1))
+        loads = ctx.enter_context(tc.tile_pool(name="loads", bufs=1))
+        work = ctx.enter_context(tc.tile_pool(name="work", bufs=2))
+        psum = ctx.enter_context(tc.psum_pool(name="psum", bufs=2))
+
+        w_ls_rows = loads.tile([P, H_TILES * H], BF16, name="w_ls_rows")
+        w_mu_rows = loads.tile([P, H_TILES * H], BF16, name="w_mu_rows")
+        x_rows = [loads.tile([P, TILES * H], BF16, name="x_rows%d" % n) for n in range(N_CHUNKS)]
+        eps_rows = [loads.tile([P, TILES * H], BF16, name="eps_rows%d" % n) for n in range(N_CHUNKS)]
+
+        def load_weight(rows, w):
+            nc.sync.dma_start(
+                out=rows[:].rearrange("p (r k) -> p r k", r=H_TILES),
+                in_=w.rearrange("(r p) k -> p r k", p=P),
+            )
+
+        load_weight(w_ls_rows, W_ls)
+        load_weight(w_mu_rows, W_mu)
+        for n in range(N_CHUNKS):
+            nc.sync.dma_start(out=x_rows[n][:], in_=x_chunks[n])
+            nc.sync.dma_start(out=eps_rows[n][:], in_=eps_chunks[n])
+
+        log_sig_c = const.tile([P, H], BF16, name="log_sig_c")
+        nc.scalar.dma_start(out=log_sig_c[:], in_=log_sigma_sq_c)
+        mu_c_rows = const.tile([P, H], BF16, name="mu_c_rows")
+        nc.scalar.dma_start(out=mu_c_rows[:], in_=mu_c)
+        bias_rows = const.tile([P, P], BF16, name="bias_rows")
+        nc.vector.memset(bias_rows[:], 0.0)
+        nc.scalar.dma_start(out=bias_rows[0:H_TILES, :], in_=b_mu.rearrange("(t p) -> t p", p=P))
+        nc.scalar.dma_start(out=bias_rows[H_TILES : 2 * H_TILES, :], in_=b_ls.rearrange("(t p) -> t p", p=P))
+
+        ident_f32 = const.tile([P, P], F32, name="ident_f32")
+        make_identity(nc, ident_f32[:])
+        ident_bf16 = const.tile([P, P], BF16, name="ident_bf16")
+        make_identity(nc, ident_bf16[:])
+
+        inv_sig = const.tile([P, H], F32, name="inv_sig")
+        nc.scalar.activation(out=inv_sig[:], in_=log_sig_c[:], func=ACT.Exp, scale=-1.0)
+        mu_inv = const.tile([P, H], F32, name="mu_inv")
+        nc.vector.tensor_tensor(out=mu_inv[:], in0=mu_c_rows[:], in1=inv_sig[:], op=ALU.mult)
+        c2_terms = const.tile([P, H], F32, name="c2_terms")
+        nc.vector.tensor_tensor(out=c2_terms[:], in0=mu_c_rows[:], in1=mu_inv[:], op=ALU.mult)
+        cluster_bf16 = const.tile([P, 2, H], BF16, name="cluster_bf16")
+        nc.scalar.copy(out=cluster_bf16[:, 0, :], in_=inv_sig[:])
+        nc.scalar.mul(out=cluster_bf16[:, 1, :], in_=mu_inv[:], mul=-2.0)
+        c2 = const.tile([P, 1], F32, name="c2")
+        nc.vector.tensor_reduce(out=c2[:], in_=c2_terms[:], axis=mybir.AxisListType.X, op=ALU.add)
+        c2_repeated = const.tile([P, P], F32, name="c2_repeated")
+        nc.vector.tensor_copy(out=c2_repeated[:], in_=c2[:, 0:1].to_broadcast([P, P]))
+
+        def scalar_copy(out, in_):
+            nc.scalar.copy(out=out, in_=in_)
+
+        def vector_copy(out, in_):
+            nc.vector.tensor_copy(out=out, in_=in_)
+
+        def flip_inputs_last(rows, copies):
+            words = rows[:].bitcast(F32)
+            grouped = work.tile([P, TILES * P * PACK], BF16, tag="grouped_in", align_bytes=64)
+            grouped_words = grouped[:].bitcast(F32).rearrange("p (i c u) -> p i c u", i=2, u=2)
+            for i in range(2):
+                flipped = psum.tile([P, 2, 2 * P], F32, tag="flip")
+                for r in range(2):
+                    for u in range(2):
+                        first = (2 * i + r) * (H // 2) + u * P
+                        nc.tensor.transpose(
+                            flipped[:, u, r * P : (r + 1) * P], words[:, first : first + P], ident_f32[:]
+                        )
+                copies[i](out=grouped_words[:, i], in_=flipped[:].rearrange("p u c -> p c u"))
+            return grouped
+
+        def quantise(grouped, codes, scales):
+            nc.vector.quantize_mx(out=codes[:].bitcast(FP8X4), scales=scales[:], in_=grouped)
+
+        w_ls_codes = const.tile([P, H], U32, name="w_ls_codes", align_bytes=64)
+        w_ls_scales = const.tile([P, H], U8, name="w_ls_scales", align_bytes=64)
+        quantise(flip_inputs_last(w_ls_rows, (scalar_copy, vector_copy))[:], w_ls_codes, w_ls_scales)
+        w_mu_codes = const.tile([P, H], U32, name="w_mu_codes", align_bytes=64)
+        w_mu_scales = const.tile([P, H], U8, name="w_mu_scales", align_bytes=64)
+        quantise(flip_inputs_last(w_mu_rows, (scalar_copy, vector_copy))[:], w_mu_codes, w_mu_scales)
+
+        bias_cols = psum.tile([P, P], BF16, tag="flip")
+        nc.tensor.transpose(bias_cols[:], bias_rows[:], ident_bf16[:])
+        b_mu_cols = const.tile([P, H_TILES], F32, name="b_mu_cols")
+        nc.vector.tensor_copy(out=b_mu_cols[:], in_=bias_cols[:, 0:H_TILES])
+        half_b_ls_cols = const.tile([P, H_TILES], F32, name="half_b_ls_cols")
+        nc.vector.tensor_scalar_mul(out=half_b_ls_cols[:], in0=bias_cols[:, H_TILES : 2 * H_TILES], scalar1=0.5)
+
+        cluster_flipped = psum.tile([P, 2, H_TILES, C], BF16, tag="flip")
+        for w in range(2):
+            for t in range(H_TILES):
+                nc.tensor.transpose(
+                    cluster_flipped[:, w, t, :], cluster_bf16[:, w, t * P : (t + 1) * P], ident_bf16[:]
+                )
+        cluster_grouped = const.tile([P, 2, C, PACK], BF16, name="cluster_grouped", align_bytes=64)
+        for w in range(2):
+            nc.scalar.copy(out=cluster_grouped[:, w], in_=cluster_flipped[:, w].rearrange("p t c -> p c t"))
+        cluster_codes = const.tile([P, 2 * C], U32, name="cluster_codes", align_bytes=64)
+        cluster_scales = const.tile([P, 2 * C], U8, name="cluster_scales", align_bytes=64)
+        quantise(cluster_grouped[:].rearrange("p w c t -> p (w c t)"), cluster_codes, cluster_scales)
+        c2_flipped = psum.tile([P, C], F32, tag="flip")
+        nc.tensor.transpose(c2_flipped[:], c2_repeated[:], ident_f32[:])
+        c2_rows = const.tile([P, C], F32, name="c2_rows")
+        nc.vector.tensor_copy(out=c2_rows[:], in_=c2_flipped[:])
+
+        x_grouped, x_mx, eps_flipped, ls_sums, mu_sums, sigma, noise = {}, {}, {}, {}, {}, {}, {}
+        z_flipped, z_grouped, zz_grouped, z_mx, zz_mx, z_rows = {}, {}, {}, {}, {}, {}
+        d_sums, d, d_min, weights, weight_sums, inverse_sums = {}, {}, {}, {}, {}, {}
+
+        def is_chunk(n):
+            return 0 <= n < N_CHUNKS
+
+        def is_step(step):
+            return 0 <= step < N_CHUNKS * H_TILES
+
+        def mx_tiles(tag):
+            codes = work.tile([P, CHUNK], U32, tag=tag + "_codes", bufs=3, align_bytes=64)
+            scales = work.tile([P, CHUNK], U8, tag=tag + "_scales", bufs=3, align_bytes=64)
+            return codes, scales
+
+        def flip_x(n):
+            if is_chunk(n):
+                x_grouped[n] = flip_inputs_last(x_rows[n], (scalar_copy, scalar_copy))
+
+        def quantise_x(n):
+            if is_chunk(n):
+                x_mx[n] = mx_tiles("x")
+                quantise(x_grouped[n][:], x_mx[n][0], x_mx[n][1])
+
+        def flip_eps(n, pair):
+            if is_chunk(n):
+                flipped = psum.tile([P, 2, CHUNK], BF16, tag="eps_flipped")
+                for i in range(2):
+                    t = 2 * pair + i
+                    for j in range(TILES):
+                        nc.tensor.transpose(
+                            flipped[:, i, j * P : (j + 1) * P],
+                            eps_rows[n][:, j * H + t * P : j * H + (t + 1) * P],
+                            ident_bf16[:],
+                        )
+                    eps_flipped[H_TILES * n + t] = flipped[:, i, :]
+
+        def first_product(step, w_codes, w_scales, tag):
+            n, t = divmod(step, H_TILES)
+            t_cols = slice(t * P, (t + 1) * P)
+            sums = psum.tile([P, CHUNK], F32, tag=tag)
+            nc.tensor.matmul_mx(
+                out=sums[:],
+                lhsT=w_codes[:, t_cols].bitcast(FP8X4),
+                lhsT_scale=w_scales[:, t_cols],
+                rhs=x_mx[n][0][:].bitcast(FP8X4),
+                rhs_scale=x_mx[n][1][:],
+                start=True,
+                stop=True,
+            )
+            return sums
+
+        def ls_product(step):
+            if is_step(step):
+                ls_sums[step] = first_product(step, w_ls_codes, w_ls_scales, "ls_sums")
+
+        def mu_product(step):
+            if is_step(step):
+                mu_sums[step] = first_product(step, w_mu_codes, w_mu_scales, "mu_sums")
+
+        def sigma_of(step):
+            if is_step(step):
+                t = step % H_TILES
+                sigma[step] = work.tile([P, CHUNK], F32, name="sigma", tag="sigma", bufs=3)
+                nc.scalar.activation(
+                    out=sigma[step][:],
+                    in_=ls_sums[step][:],
+                    func=ACT.Exp,
+                    bias=half_b_ls_cols[:, t : t + 1],
+                    scale=0.5,
+                )
+
+        def noise_of(step):
+            if is_step(step):
+                noise[step] = work.tile([P, CHUNK], F32, name="noise", tag="noise")
+                nc.vector.tensor_tensor(out=noise[step][:], in0=sigma[step][:], in1=eps_flipped[step], op=ALU.mult)
+
+        def z_of(step):
+            if is_step(step):
+                n, t = divmod(step, H_TILES)
+                if t == 0:
+                    z_flipped[n] = work.tile([P, H_TILES, CHUNK], F32, name="z_flipped", tag="z_flipped")
+                nc.vector.scalar_tensor_tensor(
+                    out=z_flipped[n][:, t, :],
+                    in0=mu_sums[step][:],
+                    scalar=b_mu_cols[:, t : t + 1],
+                    in1=noise[step][:],
+                    op0=ALU.add,
+                    op1=ALU.add,
+                )
+
+        def group_z(n):
+            if is_chunk(n):
+                z_grouped[n] = work.tile([P, CHUNK, PACK], BF16, name="z_grouped", tag="z_grouped", align_bytes=64)
+                nc.vector.tensor_copy(out=z_grouped[n][:], in_=z_flipped[n][:].rearrange("p t c -> p c t"))
+
+        def group_zz(n):
+            if is_chunk(n):
+                zz_grouped[n] = work.tile([P, CHUNK, PACK], BF16, name="zz_grouped", tag="zz_grouped", align_bytes=64)
+                nc.scalar.activation(
+                    out=zz_grouped[n][:], in_=z_flipped[n][:].rearrange("p t c -> p c t"), func=ACT.Square
+                )
+
+        def quantise_z(n):
+            if is_chunk(n):
+                z_mx[n] = mx_tiles("z")
+                quantise(z_grouped[n][:].rearrange("p c t -> p (c t)"), z_mx[n][0], z_mx[n][1])
+
+        def quantise_zz(n):
+            if is_chunk(n):
+                zz_mx[n] = mx_tiles("zz")
+                quantise(zz_grouped[n][:].rearrange("p c t -> p (c t)"), zz_mx[n][0], zz_mx[n][1])
+
+        def return_z(n, j):
+            if is_chunk(n):
+                if j == 0:
+                    z_rows[n] = work.tile([P, TILES, H], F32, name="z_rows", tag="z_rows")
+                z_back = psum.tile([P, H], F32, tag="flip")
+                for t in range(H_TILES):
+                    nc.tensor.transpose(
+                        z_back[:, t * P : (t + 1) * P], z_flipped[n][:, t, j * P : (j + 1) * P], ident_f32[:]
+                    )
+                nc.scalar.copy(out=z_rows[n][:, j, :], in_=z_back[:])
+                if j == TILES - 1:
+                    nc.sync.dma_start(out=z_chunks[n], in_=z_rows[n][:].rearrange("p j h -> p (j h)"))
+
+        def second_products(n):
+            if is_chunk(n):
+                d_sums[n] = psum.tile([P, TILES, C], F32, name="d_sums", tag="flip")
+                for j in range(TILES):
+                    j_cols = slice(j * P, (j + 1) * P)
+                    nc.tensor.matmul_mx(
+                        out=d_sums[n][:, j, :],
+                        lhsT=zz_mx[n][0][:, j_cols].bitcast(FP8X4),
+                        lhsT_scale=zz_mx[n][1][:, j_cols],
+                        rhs=cluster_codes[:, 0:C].bitcast(FP8X4),
+                        rhs_scale=cluster_scales[:, 0:C],
+                        start=True,
+                        stop=False,
+                    )
+                    nc.tensor.matmul_mx(
+                        out=d_sums[n][:, j, :],
+                        lhsT=z_mx[n][0][:, j_cols].bitcast(FP8X4),
+                        lhsT_scale=z_mx[n][1][:, j_cols],
+                        rhs=cluster_codes[:, C : 2 * C].bitcast(FP8X4),
+                        rhs_scale=cluster_scales[:, C : 2 * C],
+                        start=False,
+                        stop=True,
+                    )
+
+        def add_c2(n):
+            if is_chunk(n):
+                d[n] = work.tile([P, TILES, C], F32, name="d", tag="d")
+                nc.vector.tensor_tensor(
+                    out=d[n][:], in0=d_sums[n][:], in1=c2_rows[:].unsqueeze(1).to_broadcast([P, TILES, C]), op=ALU.add
+                )
+
+        def row_minimum(n):
+            if is_chunk(n):
+                d_min[n] = work.tile([P, TILES], F32, name="d_min", tag="d_min")
+                nc.vector.tensor_reduce(out=d_min[n][:], in_=d[n][:], axis=mybir.AxisListType.X, op=ALU.min)
+
+        def exponentials(n):
+            if is_chunk(n):
+                weights[n] = work.tile([P, TILES, C], F32, name="weights", tag="weights")
+                weight_sums[n] = work.tile([P, TILES], F32, name="weight_sums", tag="weight_sums")
+                for j in range(TILES):
+                    nc.scalar.activation(
+                        out=weights[n][:, j, :],
+                        in_=d[n][:, j, :],
+                        func=ACT.Exp,
+                        bias=d_min[n][:, j : j + 1],
+                        scale=-1.0,
+                        accum_out=weight_sums[n][:, j : j + 1],
+                    )
+
+        def invert_sums(n):
+            if is_chunk(n):
+                inverse_sums[n] = work.tile([P, TILES], F32, name="inverse_sums", tag="inverse_sums")
+                nc.vector.reciprocal(out=inverse_sums[n][:], in_=weight_sums[n][:])
+
+        def return_att(n):
+            if is_chunk(n):
+                att = work.tile([P, TILES, C], F32, tag="att")
+                for j in range(TILES):
+                    nc.vector.tensor_scalar_mul(
+                        out=att[:, j, :], in0=weights[n][:, j, :], scalar1=inverse_sums[n][:, j : j + 1]
+                    )
+                nc.sync.dma_start(out=att_chunks[n], in_=att[:].rearrange("p j c -> p (j c)"))
+
+        for step in range(-FILL_STEPS, N_CHUNKS * H_TILES + DRAIN_STEPS):
+            n, t = divmod(step, H_TILES)
+            ls_product(step + 3)
+            mu_product(step + 1)
+            sigma_of(step + 2)
+            noise_of(step + 1)
+            z_of(step)
+            if t == 0:
+                group_z(n - 1)
+                group_zz(n - 1)
+                add_c2(n - 2)
+                flip_eps(n, 1)
+                return_z(n - 1, 0)
+                return_z(n - 1, 1)
+            if t == 1:
+                row_minimum(n - 2)
+                quantise_z(n - 1)
+                return_z(n - 1, 2)
+                return_z(n - 1, 3)
+                exponentials(n - 2)
+            if t == 2:
+                quantise_zz(n - 1)
+                invert_sums(n - 2)
+                flip_eps(n + 1, 0)
+                flip_x(n + 2)
+            if t == 3:
+                second_products(n - 1)
+                return_att(n - 2)
+                quantise_x(n + 2)

@@ -21,8 +21,9 @@ TILES = CHUNK // P
 H_TILES = H // P
 N_CHUNKS = B // CHUNK
 
-FILL_STEPS = 6
-DRAIN_STEPS = 8
+BANKS = 6
+FILL_STEPS = 8
+DRAIN_STEPS = 12
 
 FLOPS = 2 * B * H * (2 * H) + 2 * B * H * (2 * C)
 
@@ -95,39 +96,44 @@ def tile_latent_pa_t_kernel(
         def vector_copy(out, in_):
             nc.vector.tensor_copy(out=out, in_=in_)
 
-        def flip_inputs_last(rows, copies):
+        def flip_words(rows, i):
             words = rows[:].bitcast(F32)
+            flipped = psum.tile([P, 2, 2 * P], F32, tag="bank", bufs=BANKS)
+            for r in range(2):
+                for u in range(2):
+                    first = (2 * i + r) * (H // 2) + u * P
+                    nc.tensor.transpose(flipped[:, u, r * P : (r + 1) * P], words[:, first : first + P], ident_f32[:])
+            return flipped
+
+        def new_grouped():
             grouped = work.tile([P, TILES * P * PACK], BF16, tag="grouped_in", align_bytes=64)
-            grouped_words = grouped[:].bitcast(F32).rearrange("p (i c u) -> p i c u", i=2, u=2)
-            for i in range(2):
-                flipped = psum.tile([P, 2, 2 * P], F32, tag="flip")
-                for r in range(2):
-                    for u in range(2):
-                        first = (2 * i + r) * (H // 2) + u * P
-                        nc.tensor.transpose(
-                            flipped[:, u, r * P : (r + 1) * P], words[:, first : first + P], ident_f32[:]
-                        )
-                copies[i](out=grouped_words[:, i], in_=flipped[:].rearrange("p u c -> p c u"))
             return grouped
+
+        def group_words(flipped, grouped, i, copy):
+            grouped_words = grouped[:].bitcast(F32).rearrange("p (i c u) -> p i c u", i=2, u=2)
+            copy(out=grouped_words[:, i], in_=flipped[:].rearrange("p u c -> p c u"))
 
         def quantise(grouped, codes, scales):
             nc.vector.quantize_mx(out=codes[:].bitcast(FP8X4), scales=scales[:], in_=grouped)
 
         w_ls_codes = const.tile([P, H], U32, name="w_ls_codes", align_bytes=64)
         w_ls_scales = const.tile([P, H], U8, name="w_ls_scales", align_bytes=64)
-        quantise(flip_inputs_last(w_ls_rows, (scalar_copy, vector_copy))[:], w_ls_codes, w_ls_scales)
         w_mu_codes = const.tile([P, H], U32, name="w_mu_codes", align_bytes=64)
         w_mu_scales = const.tile([P, H], U8, name="w_mu_scales", align_bytes=64)
-        quantise(flip_inputs_last(w_mu_rows, (scalar_copy, vector_copy))[:], w_mu_codes, w_mu_scales)
+        for rows, codes, scales in ((w_ls_rows, w_ls_codes, w_ls_scales), (w_mu_rows, w_mu_codes, w_mu_scales)):
+            w_grouped = new_grouped()
+            group_words(flip_words(rows, 0), w_grouped, 0, scalar_copy)
+            group_words(flip_words(rows, 1), w_grouped, 1, vector_copy)
+            quantise(w_grouped[:], codes, scales)
 
-        bias_cols = psum.tile([P, P], BF16, tag="flip")
+        bias_cols = psum.tile([P, P], BF16, tag="bank", bufs=BANKS)
         nc.tensor.transpose(bias_cols[:], bias_rows[:], ident_bf16[:])
         b_mu_cols = const.tile([P, H_TILES], F32, name="b_mu_cols")
         nc.vector.tensor_copy(out=b_mu_cols[:], in_=bias_cols[:, 0:H_TILES])
         half_b_ls_cols = const.tile([P, H_TILES], F32, name="half_b_ls_cols")
         nc.vector.tensor_scalar_mul(out=half_b_ls_cols[:], in0=bias_cols[:, H_TILES : 2 * H_TILES], scalar1=0.5)
 
-        cluster_flipped = psum.tile([P, 2, H_TILES, C], BF16, tag="flip")
+        cluster_flipped = psum.tile([P, 2, H_TILES, C], BF16, tag="bank", bufs=BANKS)
         for w in range(2):
             for t in range(H_TILES):
                 nc.tensor.transpose(
@@ -139,13 +145,13 @@ def tile_latent_pa_t_kernel(
         cluster_codes = const.tile([P, 2 * C], U32, name="cluster_codes", align_bytes=64)
         cluster_scales = const.tile([P, 2 * C], U8, name="cluster_scales", align_bytes=64)
         quantise(cluster_grouped[:].rearrange("p w c t -> p (w c t)"), cluster_codes, cluster_scales)
-        c2_flipped = psum.tile([P, C], F32, tag="flip")
+        c2_flipped = psum.tile([P, C], F32, tag="bank", bufs=BANKS)
         nc.tensor.transpose(c2_flipped[:], c2_repeated[:], ident_f32[:])
         c2_rows = const.tile([P, C], F32, name="c2_rows")
         nc.vector.tensor_copy(out=c2_rows[:], in_=c2_flipped[:])
 
-        x_grouped, x_mx, eps_flipped, ls_sums, mu_sums, sigma, noise = {}, {}, {}, {}, {}, {}, {}
-        z_flipped, z_grouped, zz_grouped, z_mx, zz_mx, z_rows = {}, {}, {}, {}, {}, {}
+        x_flipped, x_grouped, x_mx, eps_flipped, ls_sums, mu_sums, sigma, noise = {}, {}, {}, {}, {}, {}, {}, {}
+        z_flipped, z_grouped, zz_grouped, z_mx, zz_mx, z_back, z_rows = {}, {}, {}, {}, {}, {}, {}
         d_sums, d, d_min, weights, weight_sums, inverse_sums = {}, {}, {}, {}, {}, {}
 
         def is_chunk(n):
@@ -159,9 +165,15 @@ def tile_latent_pa_t_kernel(
             scales = work.tile([P, CHUNK], U8, tag=tag + "_scales", bufs=3, align_bytes=64)
             return codes, scales
 
-        def flip_x(n):
+        def flip_x(n, i):
             if is_chunk(n):
-                x_grouped[n] = flip_inputs_last(x_rows[n], (scalar_copy, scalar_copy))
+                x_flipped[n, i] = flip_words(x_rows[n], i)
+
+        def group_x(n, i):
+            if is_chunk(n):
+                if i == 0:
+                    x_grouped[n] = new_grouped()
+                group_words(x_flipped[n, i], x_grouped[n], i, scalar_copy)
 
         def quantise_x(n):
             if is_chunk(n):
@@ -181,10 +193,10 @@ def tile_latent_pa_t_kernel(
                         )
                     eps_flipped[H_TILES * n + t] = flipped[:, i, :]
 
-        def first_product(step, w_codes, w_scales, tag):
+        def first_product(step, w_codes, w_scales):
             n, t = divmod(step, H_TILES)
             t_cols = slice(t * P, (t + 1) * P)
-            sums = psum.tile([P, CHUNK], F32, tag=tag)
+            sums = psum.tile([P, CHUNK], F32, tag="bank", bufs=BANKS)
             nc.tensor.matmul_mx(
                 out=sums[:],
                 lhsT=w_codes[:, t_cols].bitcast(FP8X4),
@@ -198,11 +210,11 @@ def tile_latent_pa_t_kernel(
 
         def ls_product(step):
             if is_step(step):
-                ls_sums[step] = first_product(step, w_ls_codes, w_ls_scales, "ls_sums")
+                ls_sums[step] = first_product(step, w_ls_codes, w_ls_scales)
 
         def mu_product(step):
             if is_step(step):
-                mu_sums[step] = first_product(step, w_mu_codes, w_mu_scales, "mu_sums")
+                mu_sums[step] = first_product(step, w_mu_codes, w_mu_scales)
 
         def sigma_of(step):
             if is_step(step):
@@ -257,22 +269,26 @@ def tile_latent_pa_t_kernel(
                 zz_mx[n] = mx_tiles("zz")
                 quantise(zz_grouped[n][:].rearrange("p c t -> p (c t)"), zz_mx[n][0], zz_mx[n][1])
 
+        def flip_z_back(n, j):
+            if is_chunk(n):
+                z_back[n, j] = psum.tile([P, H], F32, name="z_back", tag="bank", bufs=BANKS)
+                for t in range(H_TILES):
+                    nc.tensor.transpose(
+                        z_back[n, j][:, t * P : (t + 1) * P], z_flipped[n][:, t, j * P : (j + 1) * P], ident_f32[:]
+                    )
+
         def return_z(n, j):
             if is_chunk(n):
                 if j == 0:
                     z_rows[n] = work.tile([P, TILES, H], F32, name="z_rows", tag="z_rows")
-                z_back = psum.tile([P, H], F32, tag="flip")
-                for t in range(H_TILES):
-                    nc.tensor.transpose(
-                        z_back[:, t * P : (t + 1) * P], z_flipped[n][:, t, j * P : (j + 1) * P], ident_f32[:]
-                    )
-                nc.scalar.copy(out=z_rows[n][:, j, :], in_=z_back[:])
+                copy = vector_copy if j == TILES - 1 else scalar_copy
+                copy(out=z_rows[n][:, j, :], in_=z_back[n, j][:])
                 if j == TILES - 1:
                     nc.sync.dma_start(out=z_chunks[n], in_=z_rows[n][:].rearrange("p j h -> p (j h)"))
 
         def second_products(n):
             if is_chunk(n):
-                d_sums[n] = psum.tile([P, TILES, C], F32, name="d_sums", tag="flip")
+                d_sums[n] = psum.tile([P, TILES, C], F32, name="d_sums", tag="bank", bufs=BANKS)
                 for j in range(TILES):
                     j_cols = slice(j * P, (j + 1) * P)
                     nc.tensor.matmul_mx(
@@ -336,30 +352,42 @@ def tile_latent_pa_t_kernel(
 
         for step in range(-FILL_STEPS, N_CHUNKS * H_TILES + DRAIN_STEPS):
             n, t = divmod(step, H_TILES)
-            ls_product(step + 3)
-            mu_product(step + 1)
             sigma_of(step + 2)
             noise_of(step + 1)
             z_of(step)
             if t == 0:
                 group_z(n - 1)
                 group_zz(n - 1)
-                add_c2(n - 2)
-                flip_eps(n, 1)
                 return_z(n - 1, 0)
-                return_z(n - 1, 1)
+                invert_sums(n - 3)
             if t == 1:
-                row_minimum(n - 2)
-                quantise_z(n - 1)
-                return_z(n - 1, 2)
-                return_z(n - 1, 3)
-                exponentials(n - 2)
+                add_c2(n - 2)
+                return_z(n - 1, 1)
+                group_x(n + 2, 0)
             if t == 2:
-                quantise_zz(n - 1)
-                invert_sums(n - 2)
-                flip_eps(n + 1, 0)
-                flip_x(n + 2)
+                row_minimum(n - 2)
+                return_z(n - 1, 2)
+                group_x(n + 2, 1)
             if t == 3:
-                second_products(n - 1)
-                return_att(n - 2)
+                exponentials(n - 2)
+                return_z(n - 1, 3)
                 quantise_x(n + 2)
+                quantise_z(n - 1)
+                quantise_zz(n - 1)
+                return_att(n - 3)
+
+            ls_product(step + 3)
+            mu_product(step + 1)
+            if t == 0:
+                second_products(n - 2)
+                flip_z_back(n - 1, 1)
+                flip_x(n + 2, 0)
+            if t == 1:
+                flip_eps(n + 1, 0)
+                flip_z_back(n - 1, 2)
+                flip_x(n + 2, 1)
+            if t == 2:
+                flip_z_back(n - 1, 3)
+            if t == 3:
+                flip_eps(n + 1, 1)
+                flip_z_back(n, 0)

@@ -250,14 +250,24 @@ def tile_latent_pa_t_kernel(
         def group_z(n):
             if is_chunk(n):
                 z_grouped[n] = work.tile([P, CHUNK, PACK], BF16, name="z_grouped", tag="z_grouped", align_bytes=64)
-                nc.vector.tensor_copy(out=z_grouped[n][:], in_=z_flipped[n][:].rearrange("p t c -> p c t"))
+                nc.gpsimd.tensor_scalar(
+                    out=z_grouped[n][:],
+                    in0=z_flipped[n][:].rearrange("p t c -> p c t"),
+                    scalar1=1.0,
+                    scalar2=0.0,
+                    op0=ALU.mult,
+                    op1=ALU.add,
+                )
 
         def group_zz(n):
             if is_chunk(n):
                 zz_grouped[n] = work.tile([P, CHUNK, PACK], BF16, name="zz_grouped", tag="zz_grouped", align_bytes=64)
-                nc.scalar.activation(
-                    out=zz_grouped[n][:], in_=z_flipped[n][:].rearrange("p t c -> p c t"), func=ACT.Square
+                by_row = z_flipped[n][:].rearrange("p t c -> p c t")
+                half = CHUNK // 2
+                nc.gpsimd.tensor_tensor(
+                    out=zz_grouped[n][:, half:CHUNK, :], in0=by_row[:, half:CHUNK, :], in1=by_row[:, half:CHUNK, :], op=ALU.mult
                 )
+                nc.scalar.activation(out=zz_grouped[n][:, 0:half, :], in_=by_row[:, 0:half, :], func=ACT.Square)
 
         def quantise_z(n):
             if is_chunk(n):
@@ -356,10 +366,9 @@ def tile_latent_pa_t_kernel(
             noise_of(step + 1)
             z_of(step)
             if t == 0:
-                group_z(n - 1)
                 group_zz(n - 1)
+                group_z(n - 1)
                 return_z(n - 1, 0)
-                invert_sums(n - 3)
             if t == 1:
                 add_c2(n - 2)
                 return_z(n - 1, 1)
@@ -371,6 +380,7 @@ def tile_latent_pa_t_kernel(
             if t == 3:
                 exponentials(n - 2)
                 return_z(n - 1, 3)
+                invert_sums(n - 3)
                 quantise_x(n + 2)
                 quantise_z(n - 1)
                 quantise_zz(n - 1)

@@ -10,6 +10,7 @@ U8 = mybir.dt.uint8
 FP8X4 = mybir.dt.float8_e4m3fn_x4
 ACT = mybir.ActivationFunctionType
 ALU = mybir.AluOpType
+ALONG_ROW = mybir.AxisListType.X
 
 P = 128
 PACK = 4
@@ -20,9 +21,13 @@ CHUNK = 512
 TILES = CHUNK // P
 H_TILES = H // P
 N_CHUNKS = B // CHUNK
+N_STEPS = N_CHUNKS * H_TILES
 
+EPS_BANKS = 2
 BANKS = 6
-FILL_STEPS = 8
+SHORT = 2
+LONG = 3
+FILL_STEPS = 4
 DRAIN_STEPS = 12
 
 FLOPS = 2 * B * H * (2 * H) + 2 * B * H * (2 * C)
@@ -42,23 +47,29 @@ def tile_latent_pa_t_kernel(
         ctx.enter_context(tc.manual_schedule())
         const = ctx.enter_context(tc.tile_pool(name="const", bufs=1))
         loads = ctx.enter_context(tc.tile_pool(name="loads", bufs=1))
-        work = ctx.enter_context(tc.tile_pool(name="work", bufs=2))
-        psum = ctx.enter_context(tc.psum_pool(name="psum", bufs=2))
+        work = ctx.enter_context(tc.tile_pool(name="work", bufs=SHORT))
+        psum = ctx.enter_context(tc.psum_pool(name="psum", bufs=EPS_BANKS))
+
+        def bank(shape, dtype):
+            next_bank = psum.tile(shape, dtype, tag="bank", bufs=BANKS)
+            return next_bank
 
         w_ls_rows = loads.tile([P, H_TILES * H], BF16, name="w_ls_rows")
         w_mu_rows = loads.tile([P, H_TILES * H], BF16, name="w_mu_rows")
         x_rows = [loads.tile([P, TILES * H], BF16, name="x_rows%d" % n) for n in range(N_CHUNKS)]
         eps_rows = [loads.tile([P, TILES * H], BF16, name="eps_rows%d" % n) for n in range(N_CHUNKS)]
 
-        def load_weight(rows, w):
+        def load_weight(rows, weight):
             nc.sync.dma_start(
-                out=rows[:].rearrange("p (r k) -> p r k", r=H_TILES),
-                in_=w.rearrange("(r p) k -> p r k", p=P),
+                out=rows[:].rearrange("p (t k) -> p t k", t=H_TILES),
+                in_=weight.rearrange("(t p) k -> p t k", p=P),
             )
 
+        nc.sync.dma_start(out=x_rows[0][:], in_=x_chunks[0])
         load_weight(w_ls_rows, W_ls)
         load_weight(w_mu_rows, W_mu)
-        for n in range(N_CHUNKS):
+        nc.sync.dma_start(out=eps_rows[0][:], in_=eps_chunks[0])
+        for n in range(1, N_CHUNKS):
             nc.sync.dma_start(out=x_rows[n][:], in_=x_chunks[n])
             nc.sync.dma_start(out=eps_rows[n][:], in_=eps_chunks[n])
 
@@ -86,7 +97,7 @@ def tile_latent_pa_t_kernel(
         nc.scalar.copy(out=cluster_bf16[:, 0, :], in_=inv_sig[:])
         nc.scalar.mul(out=cluster_bf16[:, 1, :], in_=mu_inv[:], mul=-2.0)
         c2 = const.tile([P, 1], F32, name="c2")
-        nc.vector.tensor_reduce(out=c2[:], in_=c2_terms[:], axis=mybir.AxisListType.X, op=ALU.add)
+        nc.vector.tensor_reduce(out=c2[:], in_=c2_terms[:], axis=ALONG_ROW, op=ALU.add)
         c2_repeated = const.tile([P, P], F32, name="c2_repeated")
         nc.vector.tensor_copy(out=c2_repeated[:], in_=c2[:, 0:1].to_broadcast([P, P]))
 
@@ -96,12 +107,12 @@ def tile_latent_pa_t_kernel(
         def vector_copy(out, in_):
             nc.vector.tensor_copy(out=out, in_=in_)
 
-        def flip_words(rows, i):
+        def flip_words(rows, half):
             words = rows[:].bitcast(F32)
-            flipped = psum.tile([P, 2, 2 * P], F32, tag="bank", bufs=BANKS)
+            flipped = bank([P, 2, 2 * P], F32)
             for r in range(2):
                 for u in range(2):
-                    first = (2 * i + r) * (H // 2) + u * P
+                    first = (2 * half + r) * (H // 2) + u * P
                     nc.tensor.transpose(flipped[:, u, r * P : (r + 1) * P], words[:, first : first + P], ident_f32[:])
             return flipped
 
@@ -109,46 +120,12 @@ def tile_latent_pa_t_kernel(
             grouped = work.tile([P, TILES * P * PACK], BF16, tag="grouped_in", align_bytes=64)
             return grouped
 
-        def group_words(flipped, grouped, i, copy):
+        def group_words(flipped, grouped, half, copy):
             grouped_words = grouped[:].bitcast(F32).rearrange("p (i c u) -> p i c u", i=2, u=2)
-            copy(out=grouped_words[:, i], in_=flipped[:].rearrange("p u c -> p c u"))
+            copy(out=grouped_words[:, half], in_=flipped[:].rearrange("p u c -> p c u"))
 
         def quantise(grouped, codes, scales):
             nc.vector.quantize_mx(out=codes[:].bitcast(FP8X4), scales=scales[:], in_=grouped)
-
-        w_ls_codes = const.tile([P, H], U32, name="w_ls_codes", align_bytes=64)
-        w_ls_scales = const.tile([P, H], U8, name="w_ls_scales", align_bytes=64)
-        w_mu_codes = const.tile([P, H], U32, name="w_mu_codes", align_bytes=64)
-        w_mu_scales = const.tile([P, H], U8, name="w_mu_scales", align_bytes=64)
-        for rows, codes, scales in ((w_ls_rows, w_ls_codes, w_ls_scales), (w_mu_rows, w_mu_codes, w_mu_scales)):
-            w_grouped = new_grouped()
-            group_words(flip_words(rows, 0), w_grouped, 0, scalar_copy)
-            group_words(flip_words(rows, 1), w_grouped, 1, vector_copy)
-            quantise(w_grouped[:], codes, scales)
-
-        bias_cols = psum.tile([P, P], BF16, tag="bank", bufs=BANKS)
-        nc.tensor.transpose(bias_cols[:], bias_rows[:], ident_bf16[:])
-        b_mu_cols = const.tile([P, H_TILES], F32, name="b_mu_cols")
-        nc.vector.tensor_copy(out=b_mu_cols[:], in_=bias_cols[:, 0:H_TILES])
-        half_b_ls_cols = const.tile([P, H_TILES], F32, name="half_b_ls_cols")
-        nc.vector.tensor_scalar_mul(out=half_b_ls_cols[:], in0=bias_cols[:, H_TILES : 2 * H_TILES], scalar1=0.5)
-
-        cluster_flipped = psum.tile([P, 2, H_TILES, C], BF16, tag="bank", bufs=BANKS)
-        for w in range(2):
-            for t in range(H_TILES):
-                nc.tensor.transpose(
-                    cluster_flipped[:, w, t, :], cluster_bf16[:, w, t * P : (t + 1) * P], ident_bf16[:]
-                )
-        cluster_grouped = const.tile([P, 2, C, PACK], BF16, name="cluster_grouped", align_bytes=64)
-        for w in range(2):
-            nc.scalar.copy(out=cluster_grouped[:, w], in_=cluster_flipped[:, w].rearrange("p t c -> p c t"))
-        cluster_codes = const.tile([P, 2 * C], U32, name="cluster_codes", align_bytes=64)
-        cluster_scales = const.tile([P, 2 * C], U8, name="cluster_scales", align_bytes=64)
-        quantise(cluster_grouped[:].rearrange("p w c t -> p (w c t)"), cluster_codes, cluster_scales)
-        c2_flipped = psum.tile([P, C], F32, tag="bank", bufs=BANKS)
-        nc.tensor.transpose(c2_flipped[:], c2_repeated[:], ident_f32[:])
-        c2_rows = const.tile([P, C], F32, name="c2_rows")
-        nc.vector.tensor_copy(out=c2_rows[:], in_=c2_flipped[:])
 
         x_flipped, x_grouped, x_mx, eps_flipped, ls_sums, mu_sums, sigma, noise = {}, {}, {}, {}, {}, {}, {}, {}
         z_flipped, z_grouped, zz_grouped, z_mx, zz_mx, z_back, z_rows = {}, {}, {}, {}, {}, {}, {}
@@ -158,22 +135,22 @@ def tile_latent_pa_t_kernel(
             return 0 <= n < N_CHUNKS
 
         def is_step(step):
-            return 0 <= step < N_CHUNKS * H_TILES
+            return 0 <= step < N_STEPS
 
         def mx_tiles(tag):
-            codes = work.tile([P, CHUNK], U32, tag=tag + "_codes", bufs=3, align_bytes=64)
-            scales = work.tile([P, CHUNK], U8, tag=tag + "_scales", bufs=3, align_bytes=64)
+            codes = work.tile([P, CHUNK], U32, tag=tag + "_codes", bufs=LONG, align_bytes=64)
+            scales = work.tile([P, CHUNK], U8, tag=tag + "_scales", bufs=LONG, align_bytes=64)
             return codes, scales
 
-        def flip_x(n, i):
+        def flip_x(n, half):
             if is_chunk(n):
-                x_flipped[n, i] = flip_words(x_rows[n], i)
+                x_flipped[n, half] = flip_words(x_rows[n], half)
 
-        def group_x(n, i):
+        def group_x(n, half):
             if is_chunk(n):
-                if i == 0:
+                if half == 0:
                     x_grouped[n] = new_grouped()
-                group_words(x_flipped[n, i], x_grouped[n], i, scalar_copy)
+                group_words(x_flipped[n, half], x_grouped[n], half, scalar_copy)
 
         def quantise_x(n):
             if is_chunk(n):
@@ -183,20 +160,20 @@ def tile_latent_pa_t_kernel(
         def flip_eps(n, pair):
             if is_chunk(n):
                 flipped = psum.tile([P, 2, CHUNK], BF16, tag="eps_flipped")
-                for i in range(2):
-                    t = 2 * pair + i
+                for side in range(2):
+                    t = 2 * pair + side
                     for j in range(TILES):
                         nc.tensor.transpose(
-                            flipped[:, i, j * P : (j + 1) * P],
+                            flipped[:, side, j * P : (j + 1) * P],
                             eps_rows[n][:, j * H + t * P : j * H + (t + 1) * P],
                             ident_bf16[:],
                         )
-                    eps_flipped[H_TILES * n + t] = flipped[:, i, :]
+                    eps_flipped[H_TILES * n + t] = flipped[:, side, :]
 
         def first_product(step, w_codes, w_scales):
             n, t = divmod(step, H_TILES)
             t_cols = slice(t * P, (t + 1) * P)
-            sums = psum.tile([P, CHUNK], F32, tag="bank", bufs=BANKS)
+            sums = bank([P, CHUNK], F32)
             nc.tensor.matmul_mx(
                 out=sums[:],
                 lhsT=w_codes[:, t_cols].bitcast(FP8X4),
@@ -219,7 +196,7 @@ def tile_latent_pa_t_kernel(
         def sigma_of(step):
             if is_step(step):
                 t = step % H_TILES
-                sigma[step] = work.tile([P, CHUNK], F32, name="sigma", tag="sigma", bufs=3)
+                sigma[step] = work.tile([P, CHUNK], F32, name="sigma", tag="sigma", bufs=LONG)
                 nc.scalar.activation(
                     out=sigma[step][:],
                     in_=ls_sums[step][:],
@@ -230,14 +207,14 @@ def tile_latent_pa_t_kernel(
 
         def noise_of(step):
             if is_step(step):
-                noise[step] = work.tile([P, CHUNK], F32, name="noise", tag="noise")
+                noise[step] = work.tile([P, CHUNK], F32, name="noise", tag="noise", bufs=LONG)
                 nc.vector.tensor_tensor(out=noise[step][:], in0=sigma[step][:], in1=eps_flipped[step], op=ALU.mult)
 
         def z_of(step):
             if is_step(step):
                 n, t = divmod(step, H_TILES)
                 if t == 0:
-                    z_flipped[n] = work.tile([P, H_TILES, CHUNK], F32, name="z_flipped", tag="z_flipped")
+                    z_flipped[n] = work.tile([P, H_TILES, CHUNK], F32, name="z_flipped", tag="z_flipped", bufs=LONG)
                 nc.vector.scalar_tensor_tensor(
                     out=z_flipped[n][:, t, :],
                     in0=mu_sums[step][:],
@@ -247,27 +224,23 @@ def tile_latent_pa_t_kernel(
                     op1=ALU.add,
                 )
 
+        def rows_by_fours(flipped):
+            return flipped.rearrange("p t (g i) -> p g t i", i=4)
+
+        def grouped_by_fours(grouped):
+            return grouped.rearrange("p (g i) t -> p g t i", i=4)
+
         def group_z(n):
             if is_chunk(n):
                 z_grouped[n] = work.tile([P, CHUNK, PACK], BF16, name="z_grouped", tag="z_grouped", align_bytes=64)
-                nc.gpsimd.tensor_scalar(
-                    out=z_grouped[n][:],
-                    in0=z_flipped[n][:].rearrange("p t c -> p c t"),
-                    scalar1=1.0,
-                    scalar2=0.0,
-                    op0=ALU.mult,
-                    op1=ALU.add,
-                )
+                nc.vector.tensor_copy(out=grouped_by_fours(z_grouped[n][:]), in_=rows_by_fours(z_flipped[n][:]))
 
         def group_zz(n):
             if is_chunk(n):
                 zz_grouped[n] = work.tile([P, CHUNK, PACK], BF16, name="zz_grouped", tag="zz_grouped", align_bytes=64)
-                by_row = z_flipped[n][:].rearrange("p t c -> p c t")
-                half = CHUNK // 2
-                nc.gpsimd.tensor_tensor(
-                    out=zz_grouped[n][:, half:CHUNK, :], in0=by_row[:, half:CHUNK, :], in1=by_row[:, half:CHUNK, :], op=ALU.mult
+                nc.scalar.activation(
+                    out=grouped_by_fours(zz_grouped[n][:]), in_=rows_by_fours(z_flipped[n][:]), func=ACT.Square
                 )
-                nc.scalar.activation(out=zz_grouped[n][:, 0:half, :], in_=by_row[:, 0:half, :], func=ACT.Square)
 
         def quantise_z(n):
             if is_chunk(n):
@@ -281,7 +254,7 @@ def tile_latent_pa_t_kernel(
 
         def flip_z_back(n, j):
             if is_chunk(n):
-                z_back[n, j] = psum.tile([P, H], F32, name="z_back", tag="bank", bufs=BANKS)
+                z_back[n, j] = bank([P, H], F32)
                 for t in range(H_TILES):
                     nc.tensor.transpose(
                         z_back[n, j][:, t * P : (t + 1) * P], z_flipped[n][:, t, j * P : (j + 1) * P], ident_f32[:]
@@ -290,15 +263,14 @@ def tile_latent_pa_t_kernel(
         def return_z(n, j):
             if is_chunk(n):
                 if j == 0:
-                    z_rows[n] = work.tile([P, TILES, H], F32, name="z_rows", tag="z_rows")
-                copy = vector_copy if j == TILES - 1 else scalar_copy
-                copy(out=z_rows[n][:, j, :], in_=z_back[n, j][:])
+                    z_rows[n] = work.tile([P, TILES, H], F32, name="z_rows", tag="z_rows", bufs=LONG)
+                nc.scalar.copy(out=z_rows[n][:, j, :], in_=z_back[n, j][:])
                 if j == TILES - 1:
                     nc.sync.dma_start(out=z_chunks[n], in_=z_rows[n][:].rearrange("p j h -> p (j h)"))
 
         def second_products(n):
             if is_chunk(n):
-                d_sums[n] = psum.tile([P, TILES, C], F32, name="d_sums", tag="bank", bufs=BANKS)
+                d_sums[n] = bank([P, TILES, C], F32)
                 for j in range(TILES):
                     j_cols = slice(j * P, (j + 1) * P)
                     nc.tensor.matmul_mx(
@@ -330,7 +302,7 @@ def tile_latent_pa_t_kernel(
         def row_minimum(n):
             if is_chunk(n):
                 d_min[n] = work.tile([P, TILES], F32, name="d_min", tag="d_min")
-                nc.vector.tensor_reduce(out=d_min[n][:], in_=d[n][:], axis=mybir.AxisListType.X, op=ALU.min)
+                nc.vector.tensor_reduce(out=d_min[n][:], in_=d[n][:], axis=ALONG_ROW, op=ALU.min)
 
         def exponentials(n):
             if is_chunk(n):
@@ -360,15 +332,57 @@ def tile_latent_pa_t_kernel(
                     )
                 nc.sync.dma_start(out=att_chunks[n], in_=att[:].rearrange("p j c -> p (j c)"))
 
-        for step in range(-FILL_STEPS, N_CHUNKS * H_TILES + DRAIN_STEPS):
+        for half in range(2):
+            flip_x(0, half)
+            group_x(0, half)
+        quantise_x(0)
+
+        w_ls_codes = const.tile([P, H], U32, name="w_ls_codes", align_bytes=64)
+        w_ls_scales = const.tile([P, H], U8, name="w_ls_scales", align_bytes=64)
+        w_mu_codes = const.tile([P, H], U32, name="w_mu_codes", align_bytes=64)
+        w_mu_scales = const.tile([P, H], U8, name="w_mu_scales", align_bytes=64)
+        for rows, codes, scales in ((w_ls_rows, w_ls_codes, w_ls_scales), (w_mu_rows, w_mu_codes, w_mu_scales)):
+            w_grouped = new_grouped()
+            group_words(flip_words(rows, 0), w_grouped, 0, scalar_copy)
+            group_words(flip_words(rows, 1), w_grouped, 1, vector_copy)
+            quantise(w_grouped[:], codes, scales)
+
+        bias_cols = bank([P, P], BF16)
+        nc.tensor.transpose(bias_cols[:], bias_rows[:], ident_bf16[:])
+        b_mu_cols = const.tile([P, H_TILES], F32, name="b_mu_cols")
+        nc.vector.tensor_copy(out=b_mu_cols[:], in_=bias_cols[:, 0:H_TILES])
+        half_b_ls_cols = const.tile([P, H_TILES], F32, name="half_b_ls_cols")
+        nc.vector.tensor_scalar_mul(out=half_b_ls_cols[:], in0=bias_cols[:, H_TILES : 2 * H_TILES], scalar1=0.5)
+
+        cluster_flipped = bank([P, 2, H_TILES, C], BF16)
+        for operand in range(2):
+            for t in range(H_TILES):
+                nc.tensor.transpose(
+                    cluster_flipped[:, operand, t, :], cluster_bf16[:, operand, t * P : (t + 1) * P], ident_bf16[:]
+                )
+        cluster_grouped = const.tile([P, 2, C, PACK], BF16, name="cluster_grouped", align_bytes=64)
+        for operand in range(2):
+            nc.scalar.copy(
+                out=cluster_grouped[:, operand], in_=cluster_flipped[:, operand].rearrange("p t c -> p c t")
+            )
+        cluster_codes = const.tile([P, 2 * C], U32, name="cluster_codes", align_bytes=64)
+        cluster_scales = const.tile([P, 2 * C], U8, name="cluster_scales", align_bytes=64)
+        quantise(cluster_grouped[:].rearrange("p o c t -> p (o c t)"), cluster_codes, cluster_scales)
+        c2_flipped = bank([P, C], F32)
+        nc.tensor.transpose(c2_flipped[:], c2_repeated[:], ident_f32[:])
+        c2_rows = const.tile([P, C], F32, name="c2_rows")
+        nc.vector.tensor_copy(out=c2_rows[:], in_=c2_flipped[:])
+
+        for step in range(-FILL_STEPS, N_STEPS + DRAIN_STEPS):
             n, t = divmod(step, H_TILES)
             sigma_of(step + 2)
             noise_of(step + 1)
             z_of(step)
             if t == 0:
-                group_zz(n - 1)
                 group_z(n - 1)
+                group_zz(n - 1)
                 return_z(n - 1, 0)
+                invert_sums(n - 3)
             if t == 1:
                 add_c2(n - 2)
                 return_z(n - 1, 1)
@@ -380,7 +394,6 @@ def tile_latent_pa_t_kernel(
             if t == 3:
                 exponentials(n - 2)
                 return_z(n - 1, 3)
-                invert_sums(n - 3)
                 quantise_x(n + 2)
                 quantise_z(n - 1)
                 quantise_zz(n - 1)

@@ -130,6 +130,7 @@ def tile_latent_pa_t_kernel(
         x_flipped, x_grouped, x_mx, eps_flipped, ls_sums, mu_sums, sigma, noise = {}, {}, {}, {}, {}, {}, {}, {}
         z_flipped, z_grouped, zz_grouped, z_mx, zz_mx, z_back, z_rows = {}, {}, {}, {}, {}, {}, {}
         d_sums, d, d_min, weights, weight_sums, inverse_sums = {}, {}, {}, {}, {}, {}
+        eps_banks = {}
 
         def is_chunk(n):
             return 0 <= n < N_CHUNKS
@@ -157,18 +158,19 @@ def tile_latent_pa_t_kernel(
                 x_mx[n] = mx_tiles("x")
                 quantise(x_grouped[n][:], x_mx[n][0], x_mx[n][1])
 
-        def flip_eps(n, pair):
+        def flip_eps(n, t):
             if is_chunk(n):
-                flipped = psum.tile([P, 2, CHUNK], BF16, tag="eps_flipped")
-                for side in range(2):
-                    t = 2 * pair + side
-                    for j in range(TILES):
-                        nc.tensor.transpose(
-                            flipped[:, side, j * P : (j + 1) * P],
-                            eps_rows[n][:, j * H + t * P : j * H + (t + 1) * P],
-                            ident_bf16[:],
-                        )
-                    eps_flipped[H_TILES * n + t] = flipped[:, side, :]
+                if t % 2 == 0:
+                    eps_banks[n, t // 2] = psum.tile([P, 2, CHUNK], BF16, name="eps_bank", tag="eps_flipped")
+                flipped = eps_banks[n, t // 2][:, t % 2, :]
+                for j in range(TILES):
+                    out = flipped[:, j * P : (j + 1) * P]
+                    eps = eps_rows[n][:, j * H + t * P : j * H + (t + 1) * P]
+                    if n == 0:
+                        nc.tensor.transpose(out, eps, ident_bf16[:])
+                    else:
+                        nc.tensor.matmul(out, lhsT=eps, rhs=ident_bf16[:], start=True, stop=True)
+                eps_flipped[H_TILES * n + t] = flipped
 
         def first_product(step, w_codes, w_scales):
             n, t = divmod(step, H_TILES)
@@ -403,6 +405,7 @@ def tile_latent_pa_t_kernel(
             mu_product(step + 1)
             if t == 0:
                 second_products(n - 2)
+                flip_eps(n, 3)
                 flip_z_back(n - 1, 1)
                 flip_x(n + 2, 0)
             if t == 1:
@@ -410,7 +413,8 @@ def tile_latent_pa_t_kernel(
                 flip_z_back(n - 1, 2)
                 flip_x(n + 2, 1)
             if t == 2:
+                flip_eps(n + 1, 1)
                 flip_z_back(n - 1, 3)
             if t == 3:
-                flip_eps(n + 1, 1)
+                flip_eps(n + 1, 2)
                 flip_z_back(n, 0)

@@ -18,9 +18,9 @@ B = 4096
 H = 512
 C = 128
 CHUNK = 512
-TILES = CHUNK // P
 H_TILES = H // P
-N_CHUNKS = B // CHUNK
+CHUNK_ROWS = [CHUNK // 2] + [CHUNK] * (B // CHUNK - 1) + [CHUNK // 2]
+N_CHUNKS = len(CHUNK_ROWS)
 N_STEPS = N_CHUNKS * H_TILES
 
 EPS_BANKS = 2
@@ -38,10 +38,21 @@ def tile_latent_pa_t_kernel(
 ):
     nc = tc.nc
 
-    x_chunks = encoder_final_state.rearrange("(n p j) k -> n p (j k)", p=P, j=TILES)
-    eps_chunks = eps_z.rearrange("(n p j) h -> n p (j h)", p=P, j=TILES)
-    z_chunks = out_0.rearrange("(n p j) h -> n p (j h)", p=P, j=TILES)
-    att_chunks = out_1.rearrange("(n p j) c -> n p (j c)", p=P, j=TILES)
+    def row_tiles(n):
+        return CHUNK_ROWS[n] // P
+
+    def chunks_of(matrix):
+        views, first = [], 0
+        for n in range(N_CHUNKS):
+            rows = matrix[first : first + CHUNK_ROWS[n], :]
+            views.append(rows.rearrange("(p j) w -> p (j w)", j=row_tiles(n)))
+            first += CHUNK_ROWS[n]
+        return views
+
+    x_chunks = chunks_of(encoder_final_state)
+    eps_chunks = chunks_of(eps_z)
+    z_chunks = chunks_of(out_0)
+    att_chunks = chunks_of(out_1)
 
     with ExitStack() as ctx:
         ctx.enter_context(tc.manual_schedule())
@@ -56,8 +67,8 @@ def tile_latent_pa_t_kernel(
 
         w_ls_rows = loads.tile([P, H_TILES * H], BF16, name="w_ls_rows")
         w_mu_rows = loads.tile([P, H_TILES * H], BF16, name="w_mu_rows")
-        x_rows = [loads.tile([P, TILES * H], BF16, name="x_rows%d" % n) for n in range(N_CHUNKS)]
-        eps_rows = [loads.tile([P, TILES * H], BF16, name="eps_rows%d" % n) for n in range(N_CHUNKS)]
+        x_rows = [loads.tile([P, row_tiles(n) * H], BF16, name="x_rows%d" % n) for n in range(N_CHUNKS)]
+        eps_rows = [loads.tile([P, row_tiles(n) * H], BF16, name="eps_rows%d" % n) for n in range(N_CHUNKS)]
 
         def load_weight(rows, weight):
             nc.sync.dma_start(
@@ -116,12 +127,12 @@ def tile_latent_pa_t_kernel(
                     nc.tensor.transpose(flipped[:, u, r * P : (r + 1) * P], words[:, first : first + P], ident_f32[:])
             return flipped
 
-        def new_grouped():
-            grouped = work.tile([P, TILES * P * PACK], BF16, tag="grouped_in", align_bytes=64)
+        def new_grouped(columns):
+            grouped = work.tile([P, columns * PACK], BF16, tag="grouped_in", align_bytes=64)
             return grouped
 
         def group_words(flipped, grouped, half, copy):
-            grouped_words = grouped[:].bitcast(F32).rearrange("p (i c u) -> p i c u", i=2, u=2)
+            grouped_words = grouped[:].bitcast(F32).rearrange("p (i c u) -> p i c u", c=2 * P, u=2)
             copy(out=grouped_words[:, half], in_=flipped[:].rearrange("p u c -> p c u"))
 
         def quantise(grouped, codes, scales):
@@ -138,32 +149,32 @@ def tile_latent_pa_t_kernel(
         def is_step(step):
             return 0 <= step < N_STEPS
 
-        def mx_tiles(tag):
-            codes = work.tile([P, CHUNK], U32, tag=tag + "_codes", bufs=LONG, align_bytes=64)
-            scales = work.tile([P, CHUNK], U8, tag=tag + "_scales", bufs=LONG, align_bytes=64)
+        def mx_tiles(tag, n):
+            codes = work.tile([P, CHUNK_ROWS[n]], U32, tag=tag + "_codes", bufs=LONG, align_bytes=64)
+            scales = work.tile([P, CHUNK_ROWS[n]], U8, tag=tag + "_scales", bufs=LONG, align_bytes=64)
             return codes, scales
 
         def flip_x(n, half):
-            if is_chunk(n):
+            if is_chunk(n) and 2 * half < row_tiles(n):
                 x_flipped[n, half] = flip_words(x_rows[n], half)
 
         def group_x(n, half):
-            if is_chunk(n):
+            if is_chunk(n) and 2 * half < row_tiles(n):
                 if half == 0:
-                    x_grouped[n] = new_grouped()
+                    x_grouped[n] = new_grouped(CHUNK_ROWS[n])
                 group_words(x_flipped[n, half], x_grouped[n], half, scalar_copy)
 
         def quantise_x(n):
             if is_chunk(n):
-                x_mx[n] = mx_tiles("x")
+                x_mx[n] = mx_tiles("x", n)
                 quantise(x_grouped[n][:], x_mx[n][0], x_mx[n][1])
 
         def flip_eps(n, t):
             if is_chunk(n):
                 if t % 2 == 0:
-                    eps_banks[n, t // 2] = psum.tile([P, 2, CHUNK], BF16, name="eps_bank", tag="eps_flipped")
+                    eps_banks[n, t // 2] = psum.tile([P, 2, CHUNK_ROWS[n]], BF16, name="eps_bank", tag="eps_flipped")
                 flipped = eps_banks[n, t // 2][:, t % 2, :]
-                for j in range(TILES):
+                for j in range(row_tiles(n)):
                     out = flipped[:, j * P : (j + 1) * P]
                     eps = eps_rows[n][:, j * H + t * P : j * H + (t + 1) * P]
                     if n == 0:
@@ -175,7 +186,7 @@ def tile_latent_pa_t_kernel(
         def first_product(step, w_codes, w_scales):
             n, t = divmod(step, H_TILES)
             t_cols = slice(t * P, (t + 1) * P)
-            sums = bank([P, CHUNK], F32)
+            sums = bank([P, CHUNK_ROWS[n]], F32)
             nc.tensor.matmul_mx(
                 out=sums[:],
                 lhsT=w_codes[:, t_cols].bitcast(FP8X4),
@@ -197,8 +208,8 @@ def tile_latent_pa_t_kernel(
 
         def sigma_of(step):
             if is_step(step):
-                t = step % H_TILES
-                sigma[step] = work.tile([P, CHUNK], F32, name="sigma", tag="sigma", bufs=LONG)
+                n, t = divmod(step, H_TILES)
+                sigma[step] = work.tile([P, CHUNK_ROWS[n]], F32, name="sigma", tag="sigma", bufs=LONG)
                 nc.scalar.activation(
                     out=sigma[step][:],
                     in_=ls_sums[step][:],
@@ -209,14 +220,14 @@ def tile_latent_pa_t_kernel(
 
         def noise_of(step):
             if is_step(step):
-                noise[step] = work.tile([P, CHUNK], F32, name="noise", tag="noise", bufs=LONG)
+                noise[step] = work.tile([P, CHUNK_ROWS[step // H_TILES]], F32, name="noise", tag="noise", bufs=LONG)
                 nc.vector.tensor_tensor(out=noise[step][:], in0=sigma[step][:], in1=eps_flipped[step], op=ALU.mult)
 
         def z_of(step):
             if is_step(step):
                 n, t = divmod(step, H_TILES)
                 if t == 0:
-                    z_flipped[n] = work.tile([P, H_TILES, CHUNK], F32, name="z_flipped", tag="z_flipped", bufs=LONG)
+                    z_flipped[n] = work.tile([P, H_TILES, CHUNK_ROWS[n]], F32, name="z_flipped", tag="z_flipped", bufs=LONG)
                 nc.vector.scalar_tensor_tensor(
                     out=z_flipped[n][:, t, :],
                     in0=mu_sums[step][:],
@@ -234,28 +245,28 @@ def tile_latent_pa_t_kernel(
 
         def group_z(n):
             if is_chunk(n):
-                z_grouped[n] = work.tile([P, CHUNK, PACK], BF16, name="z_grouped", tag="z_grouped", align_bytes=64)
+                z_grouped[n] = work.tile([P, CHUNK_ROWS[n], PACK], BF16, name="z_grouped", tag="z_grouped", align_bytes=64)
                 nc.vector.tensor_copy(out=grouped_by_fours(z_grouped[n][:]), in_=rows_by_fours(z_flipped[n][:]))
 
         def group_zz(n):
             if is_chunk(n):
-                zz_grouped[n] = work.tile([P, CHUNK, PACK], BF16, name="zz_grouped", tag="zz_grouped", align_bytes=64)
+                zz_grouped[n] = work.tile([P, CHUNK_ROWS[n], PACK], BF16, name="zz_grouped", tag="zz_grouped", align_bytes=64)
                 nc.scalar.activation(
                     out=grouped_by_fours(zz_grouped[n][:]), in_=rows_by_fours(z_flipped[n][:]), func=ACT.Square
                 )
 
         def quantise_z(n):
             if is_chunk(n):
-                z_mx[n] = mx_tiles("z")
+                z_mx[n] = mx_tiles("z", n)
                 quantise(z_grouped[n][:].rearrange("p c t -> p (c t)"), z_mx[n][0], z_mx[n][1])
 
         def quantise_zz(n):
             if is_chunk(n):
-                zz_mx[n] = mx_tiles("zz")
+                zz_mx[n] = mx_tiles("zz", n)
                 quantise(zz_grouped[n][:].rearrange("p c t -> p (c t)"), zz_mx[n][0], zz_mx[n][1])
 
         def flip_z_back(n, j):
-            if is_chunk(n):
+            if is_chunk(n) and j < row_tiles(n):
                 z_back[n, j] = bank([P, H], F32)
                 for t in range(H_TILES):
                     nc.tensor.transpose(
@@ -263,17 +274,17 @@ def tile_latent_pa_t_kernel(
                     )
 
         def return_z(n, j):
-            if is_chunk(n):
+            if is_chunk(n) and j < row_tiles(n):
                 if j == 0:
-                    z_rows[n] = work.tile([P, TILES, H], F32, name="z_rows", tag="z_rows", bufs=LONG)
+                    z_rows[n] = work.tile([P, row_tiles(n), H], F32, name="z_rows", tag="z_rows", bufs=LONG)
                 nc.scalar.copy(out=z_rows[n][:, j, :], in_=z_back[n, j][:])
-                if j == TILES - 1:
+                if j == row_tiles(n) - 1:
                     nc.sync.dma_start(out=z_chunks[n], in_=z_rows[n][:].rearrange("p j h -> p (j h)"))
 
         def second_products(n):
             if is_chunk(n):
-                d_sums[n] = bank([P, TILES, C], F32)
-                for j in range(TILES):
+                d_sums[n] = bank([P, row_tiles(n), C], F32)
+                for j in range(row_tiles(n)):
                     j_cols = slice(j * P, (j + 1) * P)
                     nc.tensor.matmul_mx(
                         out=d_sums[n][:, j, :],
@@ -296,21 +307,22 @@ def tile_latent_pa_t_kernel(
 
         def add_c2(n):
             if is_chunk(n):
-                d[n] = work.tile([P, TILES, C], F32, name="d", tag="d")
+                shape = [P, row_tiles(n), C]
+                d[n] = work.tile(shape, F32, name="d", tag="d")
                 nc.vector.tensor_tensor(
-                    out=d[n][:], in0=d_sums[n][:], in1=c2_rows[:].unsqueeze(1).to_broadcast([P, TILES, C]), op=ALU.add
+                    out=d[n][:], in0=d_sums[n][:], in1=c2_rows[:].unsqueeze(1).to_broadcast(shape), op=ALU.add
                 )
 
         def row_minimum(n):
             if is_chunk(n):
-                d_min[n] = work.tile([P, TILES], F32, name="d_min", tag="d_min")
+                d_min[n] = work.tile([P, row_tiles(n)], F32, name="d_min", tag="d_min")
                 nc.vector.tensor_reduce(out=d_min[n][:], in_=d[n][:], axis=ALONG_ROW, op=ALU.min)
 
         def exponentials(n):
             if is_chunk(n):
-                weights[n] = work.tile([P, TILES, C], F32, name="weights", tag="weights")
-                weight_sums[n] = work.tile([P, TILES], F32, name="weight_sums", tag="weight_sums")
-                for j in range(TILES):
+                weights[n] = work.tile([P, row_tiles(n), C], F32, name="weights", tag="weights")
+                weight_sums[n] = work.tile([P, row_tiles(n)], F32, name="weight_sums", tag="weight_sums")
+                for j in range(row_tiles(n)):
                     nc.scalar.activation(
                         out=weights[n][:, j, :],
                         in_=d[n][:, j, :],
@@ -322,13 +334,13 @@ def tile_latent_pa_t_kernel(
 
         def invert_sums(n):
             if is_chunk(n):
-                inverse_sums[n] = work.tile([P, TILES], F32, name="inverse_sums", tag="inverse_sums")
+                inverse_sums[n] = work.tile([P, row_tiles(n)], F32, name="inverse_sums", tag="inverse_sums")
                 nc.vector.reciprocal(out=inverse_sums[n][:], in_=weight_sums[n][:])
 
         def return_att(n):
             if is_chunk(n):
-                att = work.tile([P, TILES, C], F32, tag="att")
-                for j in range(TILES):
+                att = work.tile([P, row_tiles(n), C], F32, tag="att")
+                for j in range(row_tiles(n)):
                     nc.vector.tensor_scalar_mul(
                         out=att[:, j, :], in0=weights[n][:, j, :], scalar1=inverse_sums[n][:, j : j + 1]
                     )
@@ -344,7 +356,7 @@ def tile_latent_pa_t_kernel(
         w_mu_codes = const.tile([P, H], U32, name="w_mu_codes", align_bytes=64)
         w_mu_scales = const.tile([P, H], U8, name="w_mu_scales", align_bytes=64)
         for rows, codes, scales in ((w_ls_rows, w_ls_codes, w_ls_scales), (w_mu_rows, w_mu_codes, w_mu_scales)):
-            w_grouped = new_grouped()
+            w_grouped = new_grouped(H)
             group_words(flip_words(rows, 0), w_grouped, 0, scalar_copy)
             group_words(flip_words(rows, 1), w_grouped, 1, vector_copy)
             quantise(w_grouped[:], codes, scales)

@@ -28,7 +28,7 @@ BANKS = 6
 SHORT = 2
 LONG = 3
 FILL_STEPS = 4
-DRAIN_STEPS = 12
+DRAIN_STEPS = 11
 
 FLOPS = 2 * B * H * (2 * H) + 2 * B * H * (2 * C)
 
@@ -55,7 +55,6 @@ def tile_latent_pa_t_kernel(
     att_chunks = chunks_of(out_1)
 
     with ExitStack() as ctx:
-        ctx.enter_context(tc.manual_schedule())
         const = ctx.enter_context(tc.tile_pool(name="const", bufs=1))
         loads = ctx.enter_context(tc.tile_pool(name="loads", bufs=1))
         work = ctx.enter_context(tc.tile_pool(name="work", bufs=SHORT))
@@ -339,7 +338,7 @@ def tile_latent_pa_t_kernel(
 
         def return_att(n):
             if is_chunk(n):
-                att = work.tile([P, row_tiles(n), C], F32, tag="att")
+                att = work.tile([P, row_tiles(n), C], F32, tag="att", bufs=LONG)
                 for j in range(row_tiles(n)):
                     nc.vector.tensor_scalar_mul(
                         out=att[:, j, :], in0=weights[n][:, j, :], scalar1=inverse_sums[n][:, j : j + 1]
@@ -389,34 +388,34 @@ def tile_latent_pa_t_kernel(
 
         for step in range(-FILL_STEPS, N_STEPS + DRAIN_STEPS):
             n, t = divmod(step, H_TILES)
+            if t == 2:
+                quantise_zz(n - 1)
             sigma_of(step + 2)
             noise_of(step + 1)
             z_of(step)
             if t == 0:
-                group_z(n - 1)
                 group_zz(n - 1)
                 return_z(n - 1, 0)
-                invert_sums(n - 3)
+                group_z(n - 1)
             if t == 1:
-                add_c2(n - 2)
                 return_z(n - 1, 1)
                 group_x(n + 2, 0)
-            if t == 2:
                 row_minimum(n - 2)
+                quantise_z(n - 1)
+            if t == 2:
                 return_z(n - 1, 2)
                 group_x(n + 2, 1)
-            if t == 3:
                 exponentials(n - 2)
-                return_z(n - 1, 3)
-                quantise_x(n + 2)
-                quantise_z(n - 1)
-                quantise_zz(n - 1)
                 return_att(n - 3)
+            if t == 3:
+                return_z(n - 1, 3)
+                add_c2(n - 1)
+                quantise_x(n + 2)
+                invert_sums(n - 2)
 
             ls_product(step + 3)
             mu_product(step + 1)
             if t == 0:
-                second_products(n - 2)
                 flip_eps(n, 3)
                 flip_z_back(n - 1, 1)
                 flip_x(n + 2, 0)
@@ -425,6 +424,7 @@ def tile_latent_pa_t_kernel(
                 flip_z_back(n - 1, 2)
                 flip_x(n + 2, 1)
             if t == 2:
+                second_products(n - 1)
                 flip_eps(n + 1, 1)
                 flip_z_back(n - 1, 3)
             if t == 3:

@@ -23,6 +23,7 @@ CHUNK_ROWS = [CHUNK // 2] + [CHUNK] * (B // CHUNK - 1) + [CHUNK // 2]
 N_CHUNKS = len(CHUNK_ROWS)
 N_STEPS = N_CHUNKS * H_TILES
 
+WARM_UP = 6
 EPS_BANKS = 2
 BANKS = 6
 SHORT = 2
@@ -92,6 +93,12 @@ def tile_latent_pa_t_kernel(
         nc.scalar.dma_start(out=bias_rows[0:H_TILES, :], in_=b_mu.rearrange("(t p) -> t p", p=P))
         nc.scalar.dma_start(out=bias_rows[H_TILES : 2 * H_TILES, :], in_=b_ls.rearrange("(t p) -> t p", p=P))
 
+        zeros = const.tile([P, P], F32, name="zeros")
+        nc.vector.memset(zeros[:], 0.0)
+        zero_sums = bank([P, P], F32)
+        for i in range(WARM_UP):
+            nc.tensor.matmul(zero_sums[:], lhsT=zeros[:], rhs=zeros[:], start=True, stop=True)
+
         ident_f32 = const.tile([P, P], F32, name="ident_f32")
         make_identity(nc, ident_f32[:])
         ident_bf16 = const.tile([P, P], BF16, name="ident_bf16")
@@ -102,12 +109,10 @@ def tile_latent_pa_t_kernel(
         mu_inv = const.tile([P, H], F32, name="mu_inv")
         nc.vector.tensor_tensor(out=mu_inv[:], in0=mu_c_rows[:], in1=inv_sig[:], op=ALU.mult)
         c2_terms = const.tile([P, H], F32, name="c2_terms")
-        nc.vector.tensor_tensor(out=c2_terms[:], in0=mu_c_rows[:], in1=mu_inv[:], op=ALU.mult)
-        cluster_bf16 = const.tile([P, 2, H], BF16, name="cluster_bf16")
-        nc.scalar.copy(out=cluster_bf16[:, 0, :], in_=inv_sig[:])
-        nc.scalar.mul(out=cluster_bf16[:, 1, :], in_=mu_inv[:], mul=-2.0)
         c2 = const.tile([P, 1], F32, name="c2")
-        nc.vector.tensor_reduce(out=c2[:], in_=c2_terms[:], axis=ALONG_ROW, op=ALU.add)
+        nc.vector.scalar_tensor_tensor(
+            out=c2_terms[:], in0=mu_c_rows[:], scalar=1.0, in1=mu_inv[:], op0=ALU.mult, op1=ALU.mult, accum_out=c2[:]
+        )
         c2_repeated = const.tile([P, P], F32, name="c2_repeated")
         nc.vector.tensor_copy(out=c2_repeated[:], in_=c2[:, 0:1].to_broadcast([P, P]))
 
@@ -236,22 +241,22 @@ def tile_latent_pa_t_kernel(
                     op1=ALU.add,
                 )
 
-        def rows_by_fours(flipped):
-            return flipped.rearrange("p t (g i) -> p g t i", i=4)
+        def by_latent_tile(flipped, group):
+            return flipped.rearrange("p t (g i) -> p g t i", i=group)
 
-        def grouped_by_fours(grouped):
-            return grouped.rearrange("p (g i) t -> p g t i", i=4)
+        def by_row(grouped, group):
+            return grouped.rearrange("p (g i) t -> p g t i", i=group)
 
         def group_z(n):
             if is_chunk(n):
                 z_grouped[n] = work.tile([P, CHUNK_ROWS[n], PACK], BF16, name="z_grouped", tag="z_grouped", align_bytes=64)
-                nc.vector.tensor_copy(out=grouped_by_fours(z_grouped[n][:]), in_=rows_by_fours(z_flipped[n][:]))
+                nc.vector.tensor_copy(out=by_row(z_grouped[n][:], 2), in_=by_latent_tile(z_flipped[n][:], 2))
 
         def group_zz(n):
             if is_chunk(n):
                 zz_grouped[n] = work.tile([P, CHUNK_ROWS[n], PACK], BF16, name="zz_grouped", tag="zz_grouped", align_bytes=64)
                 nc.scalar.activation(
-                    out=grouped_by_fours(zz_grouped[n][:]), in_=rows_by_fours(z_flipped[n][:]), func=ACT.Square
+                    out=by_row(zz_grouped[n][:], 4), in_=by_latent_tile(z_flipped[n][:], 4), func=ACT.Square
                 )
 
         def quantise_z(n):
@@ -367,16 +372,13 @@ def tile_latent_pa_t_kernel(
         half_b_ls_cols = const.tile([P, H_TILES], F32, name="half_b_ls_cols")
         nc.vector.tensor_scalar_mul(out=half_b_ls_cols[:], in0=bias_cols[:, H_TILES : 2 * H_TILES], scalar1=0.5)
 
-        cluster_flipped = bank([P, 2, H_TILES, C], BF16)
-        for operand in range(2):
-            for t in range(H_TILES):
-                nc.tensor.transpose(
-                    cluster_flipped[:, operand, t, :], cluster_bf16[:, operand, t * P : (t + 1) * P], ident_bf16[:]
-                )
         cluster_grouped = const.tile([P, 2, C, PACK], BF16, name="cluster_grouped", align_bytes=64)
-        for operand in range(2):
-            nc.scalar.copy(
-                out=cluster_grouped[:, operand], in_=cluster_flipped[:, operand].rearrange("p t c -> p c t")
+        for operand, (rows, factor) in enumerate(((inv_sig, 1.0), (mu_inv, -2.0))):
+            flipped = bank([P, H_TILES, C], F32)
+            for t in range(H_TILES):
+                nc.tensor.transpose(flipped[:, t, :], rows[:, t * P : (t + 1) * P], ident_f32[:])
+            nc.scalar.mul(
+                out=cluster_grouped[:, operand], in_=flipped[:].rearrange("p t c -> p c t"), mul=factor
             )
         cluster_codes = const.tile([P, 2 * C], U32, name="cluster_codes", align_bytes=64)
         cluster_scales = const.tile([P, 2 * C], U8, name="cluster_scales", align_bytes=64)

@@ -19,7 +19,7 @@ H = 512
 C = 128
 CHUNK = 512
 H_TILES = H // P
-CHUNK_ROWS = [CHUNK // 2] + [CHUNK] * (B // CHUNK - 1) + [CHUNK // 2]
+CHUNK_ROWS = [CHUNK] * (B // CHUNK)
 N_CHUNKS = len(CHUNK_ROWS)
 N_STEPS = N_CHUNKS * H_TILES
 
@@ -76,7 +76,9 @@ def tile_latent_pa_t_kernel(
                 in_=weight.rearrange("(t p) k -> p t k", p=P),
             )
 
-        nc.sync.dma_start(out=x_rows[0][:], in_=x_chunks[0])
+        for half in range(2):
+            columns = slice(2 * half * H, 2 * (half + 1) * H)
+            nc.sync.dma_start(out=x_rows[0][:, columns], in_=x_chunks[0][:, columns])
         load_weight(w_ls_rows, W_ls)
         load_weight(w_mu_rows, W_mu)
         nc.sync.dma_start(out=eps_rows[0][:], in_=eps_chunks[0])
@@ -142,8 +144,8 @@ def tile_latent_pa_t_kernel(
         def quantise(grouped, codes, scales):
             nc.vector.quantize_mx(out=codes[:].bitcast(FP8X4), scales=scales[:], in_=grouped)
 
-        x_flipped, x_grouped, x_mx, eps_flipped, ls_sums, mu_sums, sigma, noise = {}, {}, {}, {}, {}, {}, {}, {}
-        z_flipped, z_grouped, zz_grouped, z_mx, zz_mx, z_back, z_rows = {}, {}, {}, {}, {}, {}, {}
+        x_flipped, x_grouped, x_mx, ls_sums, mu_sums, sigma, noise = {}, {}, {}, {}, {}, {}, {}
+        z_flipped, z_grouped, z_mx, z_back, z_rows = {}, {}, {}, {}, {}
         d_sums, d, d_min, weights, weight_sums, inverse_sums = {}, {}, {}, {}, {}, {}
         eps_banks = {}
 
@@ -153,9 +155,9 @@ def tile_latent_pa_t_kernel(
         def is_step(step):
             return 0 <= step < N_STEPS
 
-        def mx_tiles(tag, n):
-            codes = work.tile([P, CHUNK_ROWS[n]], U32, tag=tag + "_codes", bufs=LONG, align_bytes=64)
-            scales = work.tile([P, CHUNK_ROWS[n]], U8, tag=tag + "_scales", bufs=LONG, align_bytes=64)
+        def mx_tiles(tag, columns):
+            codes = work.tile([P, columns], U32, tag=tag + "_codes", bufs=LONG, align_bytes=64)
+            scales = work.tile([P, columns], U8, tag=tag + "_scales", bufs=LONG, align_bytes=64)
             return codes, scales
 
         def flip_x(n, half):
@@ -170,7 +172,7 @@ def tile_latent_pa_t_kernel(
 
         def quantise_x(n):
             if is_chunk(n):
-                x_mx[n] = mx_tiles("x", n)
+                x_mx[n] = mx_tiles("x", CHUNK_ROWS[n])
                 quantise(x_grouped[n][:], x_mx[n][0], x_mx[n][1])
 
         def flip_eps(n, t):
@@ -185,7 +187,6 @@ def tile_latent_pa_t_kernel(
                         nc.tensor.transpose(out, eps, ident_bf16[:])
                     else:
                         nc.tensor.matmul(out, lhsT=eps, rhs=ident_bf16[:], start=True, stop=True)
-                eps_flipped[H_TILES * n + t] = flipped
 
         def first_product(step, w_codes, w_scales):
             n, t = divmod(step, H_TILES)
@@ -213,9 +214,10 @@ def tile_latent_pa_t_kernel(
         def sigma_of(step):
             if is_step(step):
                 n, t = divmod(step, H_TILES)
-                sigma[step] = work.tile([P, CHUNK_ROWS[n]], F32, name="sigma", tag="sigma", bufs=LONG)
+                if t % 2 == 0:
+                    sigma[step // 2] = work.tile([P, 2, CHUNK_ROWS[n]], F32, name="sigma", tag="sigma", bufs=LONG)
                 nc.scalar.activation(
-                    out=sigma[step][:],
+                    out=sigma[step // 2][:, t % 2, :],
                     in_=ls_sums[step][:],
                     func=ACT.Exp,
                     bias=half_b_ls_cols[:, t : t + 1],
@@ -224,8 +226,11 @@ def tile_latent_pa_t_kernel(
 
         def noise_of(step):
             if is_step(step):
-                noise[step] = work.tile([P, CHUNK_ROWS[step // H_TILES]], F32, name="noise", tag="noise", bufs=LONG)
-                nc.vector.tensor_tensor(out=noise[step][:], in0=sigma[step][:], in1=eps_flipped[step], op=ALU.mult)
+                n, t = divmod(step, H_TILES)
+                noise[step // 2] = work.tile([P, 2, CHUNK_ROWS[n]], F32, name="noise", tag="noise", bufs=LONG)
+                nc.vector.tensor_tensor(
+                    out=noise[step // 2][:], in0=sigma[step // 2][:], in1=eps_banks[n, t // 2][:], op=ALU.mult
+                )
 
         def z_of(step):
             if is_step(step):
@@ -236,7 +241,7 @@ def tile_latent_pa_t_kernel(
                     out=z_flipped[n][:, t, :],
                     in0=mu_sums[step][:],
                     scalar=b_mu_cols[:, t : t + 1],
-                    in1=noise[step][:],
+                    in1=noise[step // 2][:, t % 2, :],
                     op0=ALU.add,
                     op1=ALU.add,
                 )
@@ -247,27 +252,35 @@ def tile_latent_pa_t_kernel(
         def by_row(grouped, group):
             return grouped.rearrange("p (g i) t -> p g t i", i=group)
 
+        def part_tiles(n):
+            return row_tiles(n) // 2 if n == N_CHUNKS - 1 else row_tiles(n)
+
+        def parts_of(n):
+            return range(row_tiles(n) // part_tiles(n)) if is_chunk(n) else range(0)
+
+        def part_rows(n, part):
+            return slice(part * part_tiles(n) * P, (part + 1) * part_tiles(n) * P)
+
         def group_z(n):
-            if is_chunk(n):
-                z_grouped[n] = work.tile([P, CHUNK_ROWS[n], PACK], BF16, name="z_grouped", tag="z_grouped", align_bytes=64)
-                nc.vector.tensor_copy(out=by_row(z_grouped[n][:], 2), in_=by_latent_tile(z_flipped[n][:], 2))
+            for part in parts_of(n):
+                grouped = work.tile(
+                    [P, 2, part_tiles(n) * P, PACK], BF16, name="z_grouped", tag="z_grouped", align_bytes=64
+                )
+                z_part = z_flipped[n][:, :, part_rows(n, part)]
+                nc.vector.tensor_copy(out=by_row(grouped[:, 0], 2), in_=by_latent_tile(z_part, 2))
+                z_grouped[n, part] = grouped
 
         def group_zz(n):
-            if is_chunk(n):
-                zz_grouped[n] = work.tile([P, CHUNK_ROWS[n], PACK], BF16, name="zz_grouped", tag="zz_grouped", align_bytes=64)
+            for part in parts_of(n):
+                z_part = z_flipped[n][:, :, part_rows(n, part)]
                 nc.scalar.activation(
-                    out=by_row(zz_grouped[n][:], 4), in_=by_latent_tile(z_flipped[n][:], 4), func=ACT.Square
+                    out=by_row(z_grouped[n, part][:, 1], 4), in_=by_latent_tile(z_part, 4), func=ACT.Square
                 )
 
         def quantise_z(n):
-            if is_chunk(n):
-                z_mx[n] = mx_tiles("z", n)
-                quantise(z_grouped[n][:].rearrange("p c t -> p (c t)"), z_mx[n][0], z_mx[n][1])
-
-        def quantise_zz(n):
-            if is_chunk(n):
-                zz_mx[n] = mx_tiles("zz", n)
-                quantise(zz_grouped[n][:].rearrange("p c t -> p (c t)"), zz_mx[n][0], zz_mx[n][1])
+            for part in parts_of(n):
+                z_mx[n, part] = mx_tiles("z", 2 * part_tiles(n) * P)
+                quantise(z_grouped[n, part][:].rearrange("p o c t -> p (o c t)"), z_mx[n, part][0], z_mx[n, part][1])
 
         def flip_z_back(n, j):
             if is_chunk(n) and j < row_tiles(n):
@@ -282,73 +295,84 @@ def tile_latent_pa_t_kernel(
                 if j == 0:
                     z_rows[n] = work.tile([P, row_tiles(n), H], F32, name="z_rows", tag="z_rows", bufs=LONG)
                 nc.scalar.copy(out=z_rows[n][:, j, :], in_=z_back[n, j][:])
-                if j == row_tiles(n) - 1:
-                    nc.sync.dma_start(out=z_chunks[n], in_=z_rows[n][:].rearrange("p j h -> p (j h)"))
+                if (j + 1) % part_tiles(n) == 0:
+                    first = j + 1 - part_tiles(n)
+                    nc.sync.dma_start(
+                        out=z_chunks[n][:, first * H : (j + 1) * H],
+                        in_=z_rows[n][:, first : j + 1, :].rearrange("p j h -> p (j h)"),
+                    )
 
         def second_products(n):
-            if is_chunk(n):
-                d_sums[n] = bank([P, row_tiles(n), C], F32)
-                for j in range(row_tiles(n)):
-                    j_cols = slice(j * P, (j + 1) * P)
+            for part in parts_of(n):
+                codes, scales = z_mx[n, part]
+                sums = bank([P, part_tiles(n), C], F32)
+                for j in range(part_tiles(n)):
+                    z_cols = slice(j * P, (j + 1) * P)
+                    zz_cols = slice((part_tiles(n) + j) * P, (part_tiles(n) + j + 1) * P)
                     nc.tensor.matmul_mx(
-                        out=d_sums[n][:, j, :],
-                        lhsT=zz_mx[n][0][:, j_cols].bitcast(FP8X4),
-                        lhsT_scale=zz_mx[n][1][:, j_cols],
+                        out=sums[:, j, :],
+                        lhsT=codes[:, zz_cols].bitcast(FP8X4),
+                        lhsT_scale=scales[:, zz_cols],
                         rhs=cluster_codes[:, 0:C].bitcast(FP8X4),
                         rhs_scale=cluster_scales[:, 0:C],
                         start=True,
                         stop=False,
                     )
                     nc.tensor.matmul_mx(
-                        out=d_sums[n][:, j, :],
-                        lhsT=z_mx[n][0][:, j_cols].bitcast(FP8X4),
-                        lhsT_scale=z_mx[n][1][:, j_cols],
+                        out=sums[:, j, :],
+                        lhsT=codes[:, z_cols].bitcast(FP8X4),
+                        lhsT_scale=scales[:, z_cols],
                         rhs=cluster_codes[:, C : 2 * C].bitcast(FP8X4),
                         rhs_scale=cluster_scales[:, C : 2 * C],
                         start=False,
                         stop=True,
                     )
+                d_sums[n, part] = sums
 
         def add_c2(n):
-            if is_chunk(n):
-                shape = [P, row_tiles(n), C]
-                d[n] = work.tile(shape, F32, name="d", tag="d")
+            for part in parts_of(n):
+                shape = [P, part_tiles(n), C]
+                d[n, part] = work.tile(shape, F32, name="d", tag="d")
                 nc.vector.tensor_tensor(
-                    out=d[n][:], in0=d_sums[n][:], in1=c2_rows[:].unsqueeze(1).to_broadcast(shape), op=ALU.add
+                    out=d[n, part][:],
+                    in0=d_sums[n, part][:],
+                    in1=c2_rows[:].unsqueeze(1).to_broadcast(shape),
+                    op=ALU.add,
                 )
 
         def row_minimum(n):
-            if is_chunk(n):
-                d_min[n] = work.tile([P, row_tiles(n)], F32, name="d_min", tag="d_min")
-                nc.vector.tensor_reduce(out=d_min[n][:], in_=d[n][:], axis=ALONG_ROW, op=ALU.min)
+            for part in parts_of(n):
+                d_min[n, part] = work.tile([P, part_tiles(n)], F32, name="d_min", tag="d_min")
+                nc.vector.tensor_reduce(out=d_min[n, part][:], in_=d[n, part][:], axis=ALONG_ROW, op=ALU.min)
 
         def exponentials(n):
-            if is_chunk(n):
-                weights[n] = work.tile([P, row_tiles(n), C], F32, name="weights", tag="weights")
-                weight_sums[n] = work.tile([P, row_tiles(n)], F32, name="weight_sums", tag="weight_sums")
-                for j in range(row_tiles(n)):
+            for part in parts_of(n):
+                weights[n, part] = work.tile([P, part_tiles(n), C], F32, name="weights", tag="weights")
+                weight_sums[n, part] = work.tile([P, part_tiles(n)], F32, name="weight_sums", tag="weight_sums")
+                for j in range(part_tiles(n)):
                     nc.scalar.activation(
-                        out=weights[n][:, j, :],
-                        in_=d[n][:, j, :],
+                        out=weights[n, part][:, j, :],
+                        in_=d[n, part][:, j, :],
                         func=ACT.Exp,
-                        bias=d_min[n][:, j : j + 1],
+                        bias=d_min[n, part][:, j : j + 1],
                         scale=-1.0,
-                        accum_out=weight_sums[n][:, j : j + 1],
+                        accum_out=weight_sums[n, part][:, j : j + 1],
                     )
 
         def invert_sums(n):
-            if is_chunk(n):
-                inverse_sums[n] = work.tile([P, row_tiles(n)], F32, name="inverse_sums", tag="inverse_sums")
-                nc.vector.reciprocal(out=inverse_sums[n][:], in_=weight_sums[n][:])
+            for part in parts_of(n):
+                inverse_sums[n, part] = work.tile([P, part_tiles(n)], F32, name="inverse_sums", tag="inverse_sums")
+                nc.vector.reciprocal(out=inverse_sums[n, part][:], in_=weight_sums[n, part][:])
 
         def return_att(n):
-            if is_chunk(n):
-                att = work.tile([P, row_tiles(n), C], F32, tag="att", bufs=LONG)
-                for j in range(row_tiles(n)):
+            for part in parts_of(n):
+                att = work.tile([P, part_tiles(n), C], F32, name="att", tag="att", bufs=LONG)
+                for j in range(part_tiles(n)):
                     nc.vector.tensor_scalar_mul(
-                        out=att[:, j, :], in0=weights[n][:, j, :], scalar1=inverse_sums[n][:, j : j + 1]
+                        out=att[:, j, :], in0=weights[n, part][:, j, :], scalar1=inverse_sums[n, part][:, j : j + 1]
                     )
-                nc.sync.dma_start(out=att_chunks[n], in_=att[:].rearrange("p j c -> p (j c)"))
+                columns = slice(part * part_tiles(n) * C, (part + 1) * part_tiles(n) * C)
+                nc.sync.dma_start(out=att_chunks[n][:, columns], in_=att[:].rearrange("p j c -> p (j c)"))
 
         for half in range(2):
             flip_x(0, half)
@@ -362,7 +386,7 @@ def tile_latent_pa_t_kernel(
         for rows, codes, scales in ((w_ls_rows, w_ls_codes, w_ls_scales), (w_mu_rows, w_mu_codes, w_mu_scales)):
             w_grouped = new_grouped(H)
             group_words(flip_words(rows, 0), w_grouped, 0, scalar_copy)
-            group_words(flip_words(rows, 1), w_grouped, 1, vector_copy)
+            group_words(flip_words(rows, 1), w_grouped, 1, scalar_copy)
             quantise(w_grouped[:], codes, scales)
 
         bias_cols = bank([P, P], BF16)
@@ -390,45 +414,46 @@ def tile_latent_pa_t_kernel(
 
         for step in range(-FILL_STEPS, N_STEPS + DRAIN_STEPS):
             n, t = divmod(step, H_TILES)
+            if t == 0 and n >= 0:
+                quantise_x(n + 1)
             if t == 2:
-                quantise_zz(n - 1)
-            sigma_of(step + 2)
-            noise_of(step + 1)
+                quantise_z(n - 1)
+            sigma_of(step + 3)
+            if t % 2 == 1:
+                noise_of(step + 1)
             z_of(step)
             if t == 0:
+                group_z(n - 1)
                 group_zz(n - 1)
                 return_z(n - 1, 0)
-                group_z(n - 1)
             if t == 1:
                 return_z(n - 1, 1)
-                group_x(n + 2, 0)
                 row_minimum(n - 2)
-                quantise_z(n - 1)
             if t == 2:
                 return_z(n - 1, 2)
-                group_x(n + 2, 1)
+                group_x(n + 2, 0)
                 exponentials(n - 2)
                 return_att(n - 3)
             if t == 3:
                 return_z(n - 1, 3)
+                group_x(n + 2, 1)
                 add_c2(n - 1)
-                quantise_x(n + 2)
                 invert_sums(n - 2)
 
-            ls_product(step + 3)
             mu_product(step + 1)
+            ls_product(step + 4)
             if t == 0:
                 flip_eps(n, 3)
                 flip_z_back(n - 1, 1)
-                flip_x(n + 2, 0)
             if t == 1:
                 flip_eps(n + 1, 0)
                 flip_z_back(n - 1, 2)
-                flip_x(n + 2, 1)
+                flip_x(n + 2, 0)
             if t == 2:
-                second_products(n - 1)
                 flip_eps(n + 1, 1)
                 flip_z_back(n - 1, 3)
+                flip_x(n + 2, 1)
+                second_products(n - 1)
             if t == 3:
                 flip_eps(n + 1, 2)
                 flip_z_back(n, 0)

from contextlib import ExitStack

import concourse.mybir as mybir
from concourse.masks import make_identity

F32 = mybir.dt.float32
BF16 = mybir.dt.bfloat16
U32 = mybir.dt.uint32
U8 = mybir.dt.uint8
FP8X4 = mybir.dt.float8_e4m3fn_x4
ACT = mybir.ActivationFunctionType
ALU = mybir.AluOpType
ALONG_ROW = mybir.AxisListType.X

P = 128
PACK = 4
B = 4096
H = 512
C = 128
CHUNK = 512
H_TILES = H // P
CHUNK_ROWS = [CHUNK] * (B // CHUNK)
N_CHUNKS = len(CHUNK_ROWS)
N_STEPS = N_CHUNKS * H_TILES

WARM_UP = 6
EPS_BANKS = 2
BANKS = 6
SHORT = 2
LONG = 3
FILL_STEPS = 4
DRAIN_STEPS = 11

FLOPS = 2 * B * H * (2 * H) + 2 * B * H * (2 * C)


def tile_latent_pa_t_kernel(
    tc, encoder_final_state, W_mu, b_mu, W_ls, b_ls, mu_c, log_sigma_sq_c, eps_z, out_0, out_1
):
    nc = tc.nc

    def row_tiles(n):
        return CHUNK_ROWS[n] // P

    def chunks_of(matrix):
        views, first = [], 0
        for n in range(N_CHUNKS):
            rows = matrix[first : first + CHUNK_ROWS[n], :]
            views.append(rows.rearrange("(p j) w -> p (j w)", j=row_tiles(n)))
            first += CHUNK_ROWS[n]
        return views

    x_chunks = chunks_of(encoder_final_state)
    eps_chunks = chunks_of(eps_z)
    z_chunks = chunks_of(out_0)
    att_chunks = chunks_of(out_1)

    with ExitStack() as ctx:
        const = ctx.enter_context(tc.tile_pool(name="const", bufs=1))
        loads = ctx.enter_context(tc.tile_pool(name="loads", bufs=1))
        work = ctx.enter_context(tc.tile_pool(name="work", bufs=SHORT))
        psum = ctx.enter_context(tc.psum_pool(name="psum", bufs=EPS_BANKS))

        def bank(shape, dtype):
            next_bank = psum.tile(shape, dtype, tag="bank", bufs=BANKS)
            return next_bank

        w_ls_rows = loads.tile([P, H_TILES * H], BF16, name="w_ls_rows")
        w_mu_rows = loads.tile([P, H_TILES * H], BF16, name="w_mu_rows")
        x_rows = [loads.tile([P, row_tiles(n) * H], BF16, name="x_rows%d" % n) for n in range(N_CHUNKS)]
        eps_rows = [loads.tile([P, row_tiles(n) * H], BF16, name="eps_rows%d" % n) for n in range(N_CHUNKS)]

        def load_weight(rows, weight):
            nc.sync.dma_start(
                out=rows[:].rearrange("p (t k) -> p t k", t=H_TILES),
                in_=weight.rearrange("(t p) k -> p t k", p=P),
            )

        for half in range(2):
            columns = slice(2 * half * H, 2 * (half + 1) * H)
            nc.sync.dma_start(out=x_rows[0][:, columns], in_=x_chunks[0][:, columns])
        load_weight(w_ls_rows, W_ls)
        load_weight(w_mu_rows, W_mu)
        nc.sync.dma_start(out=eps_rows[0][:], in_=eps_chunks[0])
        for n in range(1, N_CHUNKS):
            nc.sync.dma_start(out=x_rows[n][:], in_=x_chunks[n])
            nc.sync.dma_start(out=eps_rows[n][:], in_=eps_chunks[n])

        log_sig_c = const.tile([P, H], BF16, name="log_sig_c")
        nc.scalar.dma_start(out=log_sig_c[:], in_=log_sigma_sq_c)
        mu_c_rows = const.tile([P, H], BF16, name="mu_c_rows")
        nc.scalar.dma_start(out=mu_c_rows[:], in_=mu_c)
        bias_rows = const.tile([P, P], BF16, name="bias_rows")
        nc.vector.memset(bias_rows[:], 0.0)
        nc.scalar.dma_start(out=bias_rows[0:H_TILES, :], in_=b_mu.rearrange("(t p) -> t p", p=P))
        nc.scalar.dma_start(out=bias_rows[H_TILES : 2 * H_TILES, :], in_=b_ls.rearrange("(t p) -> t p", p=P))

        zeros = const.tile([P, P], F32, name="zeros")
        nc.vector.memset(zeros[:], 0.0)
        zero_sums = bank([P, P], F32)
        for i in range(WARM_UP):
            nc.tensor.matmul(zero_sums[:], lhsT=zeros[:], rhs=zeros[:], start=True, stop=True)

        ident_f32 = const.tile([P, P], F32, name="ident_f32")
        make_identity(nc, ident_f32[:])
        ident_bf16 = const.tile([P, P], BF16, name="ident_bf16")
        make_identity(nc, ident_bf16[:])

        inv_sig = const.tile([P, H], F32, name="inv_sig")
        nc.scalar.activation(out=inv_sig[:], in_=log_sig_c[:], func=ACT.Exp, scale=-1.0)
        mu_inv = const.tile([P, H], F32, name="mu_inv")
        nc.vector.tensor_tensor(out=mu_inv[:], in0=mu_c_rows[:], in1=inv_sig[:], op=ALU.mult)
        c2_terms = const.tile([P, H], F32, name="c2_terms")
        c2 = const.tile([P, 1], F32, name="c2")
        nc.vector.scalar_tensor_tensor(
            out=c2_terms[:], in0=mu_c_rows[:], scalar=1.0, in1=mu_inv[:], op0=ALU.mult, op1=ALU.mult, accum_out=c2[:]
        )
        c2_repeated = const.tile([P, P], F32, name="c2_repeated")
        nc.vector.tensor_copy(out=c2_repeated[:], in_=c2[:, 0:1].to_broadcast([P, P]))

        def scalar_copy(out, in_):
            nc.scalar.copy(out=out, in_=in_)

        def vector_copy(out, in_):
            nc.vector.tensor_copy(out=out, in_=in_)

        def flip_words(rows, half):
            words = rows[:].bitcast(F32)
            flipped = bank([P, 2, 2 * P], F32)
            for r in range(2):
                for u in range(2):
                    first = (2 * half + r) * (H // 2) + u * P
                    nc.tensor.transpose(flipped[:, u, r * P : (r + 1) * P], words[:, first : first + P], ident_f32[:])
            return flipped

        def new_grouped(columns):
            grouped = work.tile([P, columns * PACK], BF16, tag="grouped_in", align_bytes=64)
            return grouped

        def group_words(flipped, grouped, half, copy):
            grouped_words = grouped[:].bitcast(F32).rearrange("p (i c u) -> p i c u", c=2 * P, u=2)
            copy(out=grouped_words[:, half], in_=flipped[:].rearrange("p u c -> p c u"))

        def quantise(grouped, codes, scales):
            nc.vector.quantize_mx(out=codes[:].bitcast(FP8X4), scales=scales[:], in_=grouped)

        x_flipped, x_grouped, x_mx, ls_sums, mu_sums, sigma, noise = {}, {}, {}, {}, {}, {}, {}
        z_flipped, z_grouped, z_mx, z_back, z_rows = {}, {}, {}, {}, {}
        d_sums, d, d_min, weights, weight_sums, inverse_sums = {}, {}, {}, {}, {}, {}
        eps_banks = {}

        def is_chunk(n):
            return 0 <= n < N_CHUNKS

        def is_step(step):
            return 0 <= step < N_STEPS

        def mx_tiles(tag, columns):
            codes = work.tile([P, columns], U32, tag=tag + "_codes", bufs=LONG, align_bytes=64)
            scales = work.tile([P, columns], U8, tag=tag + "_scales", bufs=LONG, align_bytes=64)
            return codes, scales

        def flip_x(n, half):
            if is_chunk(n) and 2 * half < row_tiles(n):
                x_flipped[n, half] = flip_words(x_rows[n], half)

        def group_x(n, half):
            if is_chunk(n) and 2 * half < row_tiles(n):
                if half == 0:
                    x_grouped[n] = new_grouped(CHUNK_ROWS[n])
                group_words(x_flipped[n, half], x_grouped[n], half, scalar_copy)

        def quantise_x(n):
            if is_chunk(n):
                x_mx[n] = mx_tiles("x", CHUNK_ROWS[n])
                quantise(x_grouped[n][:], x_mx[n][0], x_mx[n][1])

        def flip_eps(n, t):
            if is_chunk(n):
                if t % 2 == 0:
                    eps_banks[n, t // 2] = psum.tile([P, 2, CHUNK_ROWS[n]], BF16, name="eps_bank", tag="eps_flipped")
                flipped = eps_banks[n, t // 2][:, t % 2, :]
                for j in range(row_tiles(n)):
                    out = flipped[:, j * P : (j + 1) * P]
                    eps = eps_rows[n][:, j * H + t * P : j * H + (t + 1) * P]
                    if n == 0:
                        nc.tensor.transpose(out, eps, ident_bf16[:])
                    else:
                        nc.tensor.matmul(out, lhsT=eps, rhs=ident_bf16[:], start=True, stop=True)

        def first_product(step, w_codes, w_scales):
            n, t = divmod(step, H_TILES)
            t_cols = slice(t * P, (t + 1) * P)
            sums = bank([P, CHUNK_ROWS[n]], F32)
            nc.tensor.matmul_mx(
                out=sums[:],
                lhsT=w_codes[:, t_cols].bitcast(FP8X4),
                lhsT_scale=w_scales[:, t_cols],
                rhs=x_mx[n][0][:].bitcast(FP8X4),
                rhs_scale=x_mx[n][1][:],
                start=True,
                stop=True,
            )
            return sums

        def ls_product(step):
            if is_step(step):
                ls_sums[step] = first_product(step, w_ls_codes, w_ls_scales)

        def mu_product(step):
            if is_step(step):
                mu_sums[step] = first_product(step, w_mu_codes, w_mu_scales)

        def sigma_of(step):
            if is_step(step):
                n, t = divmod(step, H_TILES)
                if t % 2 == 0:
                    sigma[step // 2] = work.tile([P, 2, CHUNK_ROWS[n]], F32, name="sigma", tag="sigma", bufs=LONG)
                nc.scalar.activation(
                    out=sigma[step // 2][:, t % 2, :],
                    in_=ls_sums[step][:],
                    func=ACT.Exp,
                    bias=half_b_ls_cols[:, t : t + 1],
                    scale=0.5,
                )

        def noise_of(step):
            if is_step(step):
                n, t = divmod(step, H_TILES)
                noise[step // 2] = work.tile([P, 2, CHUNK_ROWS[n]], F32, name="noise", tag="noise", bufs=LONG)
                nc.vector.tensor_tensor(
                    out=noise[step // 2][:], in0=sigma[step // 2][:], in1=eps_banks[n, t // 2][:], op=ALU.mult
                )

        def z_of(step):
            if is_step(step):
                n, t = divmod(step, H_TILES)
                if t == 0:
                    z_flipped[n] = work.tile([P, H_TILES, CHUNK_ROWS[n]], F32, name="z_flipped", tag="z_flipped", bufs=LONG)
                nc.vector.scalar_tensor_tensor(
                    out=z_flipped[n][:, t, :],
                    in0=mu_sums[step][:],
                    scalar=b_mu_cols[:, t : t + 1],
                    in1=noise[step // 2][:, t % 2, :],
                    op0=ALU.add,
                    op1=ALU.add,
                )

        def by_latent_tile(flipped, group):
            return flipped.rearrange("p t (g i) -> p g t i", i=group)

        def by_row(grouped, group):
            return grouped.rearrange("p (g i) t -> p g t i", i=group)

        def part_tiles(n):
            return row_tiles(n) // 2 if n == N_CHUNKS - 1 else row_tiles(n)

        def parts_of(n):
            return range(row_tiles(n) // part_tiles(n)) if is_chunk(n) else range(0)

        def part_rows(n, part):
            return slice(part * part_tiles(n) * P, (part + 1) * part_tiles(n) * P)

        def group_z(n):
            for part in parts_of(n):
                grouped = work.tile(
                    [P, 2, part_tiles(n) * P, PACK], BF16, name="z_grouped", tag="z_grouped", align_bytes=64
                )
                z_part = z_flipped[n][:, :, part_rows(n, part)]
                nc.vector.tensor_copy(out=by_row(grouped[:, 0], 2), in_=by_latent_tile(z_part, 2))
                z_grouped[n, part] = grouped

        def group_zz(n):
            for part in parts_of(n):
                z_part = z_flipped[n][:, :, part_rows(n, part)]
                nc.scalar.activation(
                    out=by_row(z_grouped[n, part][:, 1], 4), in_=by_latent_tile(z_part, 4), func=ACT.Square
                )

        def quantise_z(n):
            for part in parts_of(n):
                z_mx[n, part] = mx_tiles("z", 2 * part_tiles(n) * P)
                quantise(z_grouped[n, part][:].rearrange("p o c t -> p (o c t)"), z_mx[n, part][0], z_mx[n, part][1])

        def flip_z_back(n, j):
            if is_chunk(n) and j < row_tiles(n):
                z_back[n, j] = bank([P, H], F32)
                for t in range(H_TILES):
                    nc.tensor.transpose(
                        z_back[n, j][:, t * P : (t + 1) * P], z_flipped[n][:, t, j * P : (j + 1) * P], ident_f32[:]
                    )

        def return_z(n, j):
            if is_chunk(n) and j < row_tiles(n):
                if j == 0:
                    z_rows[n] = work.tile([P, row_tiles(n), H], F32, name="z_rows", tag="z_rows", bufs=LONG)
                nc.scalar.copy(out=z_rows[n][:, j, :], in_=z_back[n, j][:])
                if (j + 1) % part_tiles(n) == 0:
                    first = j + 1 - part_tiles(n)
                    nc.sync.dma_start(
                        out=z_chunks[n][:, first * H : (j + 1) * H],
                        in_=z_rows[n][:, first : j + 1, :].rearrange("p j h -> p (j h)"),
                    )

        def second_products(n):
            for part in parts_of(n):
                codes, scales = z_mx[n, part]
                sums = bank([P, part_tiles(n), C], F32)
                for j in range(part_tiles(n)):
                    z_cols = slice(j * P, (j + 1) * P)
                    zz_cols = slice((part_tiles(n) + j) * P, (part_tiles(n) + j + 1) * P)
                    nc.tensor.matmul_mx(
                        out=sums[:, j, :],
                        lhsT=codes[:, zz_cols].bitcast(FP8X4),
                        lhsT_scale=scales[:, zz_cols],
                        rhs=cluster_codes[:, 0:C].bitcast(FP8X4),
                        rhs_scale=cluster_scales[:, 0:C],
                        start=True,
                        stop=False,
                    )
                    nc.tensor.matmul_mx(
                        out=sums[:, j, :],
                        lhsT=codes[:, z_cols].bitcast(FP8X4),
                        lhsT_scale=scales[:, z_cols],
                        rhs=cluster_codes[:, C : 2 * C].bitcast(FP8X4),
                        rhs_scale=cluster_scales[:, C : 2 * C],
                        start=False,
                        stop=True,
                    )
                d_sums[n, part] = sums

        def add_c2(n):
            for part in parts_of(n):
                shape = [P, part_tiles(n), C]
                d[n, part] = work.tile(shape, F32, name="d", tag="d")
                nc.vector.tensor_tensor(
                    out=d[n, part][:],
                    in0=d_sums[n, part][:],
                    in1=c2_rows[:].unsqueeze(1).to_broadcast(shape),
                    op=ALU.add,
                )

        def row_minimum(n):
            for part in parts_of(n):
                d_min[n, part] = work.tile([P, part_tiles(n)], F32, name="d_min", tag="d_min")
                nc.vector.tensor_reduce(out=d_min[n, part][:], in_=d[n, part][:], axis=ALONG_ROW, op=ALU.min)

        def exponentials(n):
            for part in parts_of(n):
                weights[n, part] = work.tile([P, part_tiles(n), C], F32, name="weights", tag="weights")
                weight_sums[n, part] = work.tile([P, part_tiles(n)], F32, name="weight_sums", tag="weight_sums")
                for j in range(part_tiles(n)):
                    nc.scalar.activation(
                        out=weights[n, part][:, j, :],
                        in_=d[n, part][:, j, :],
                        func=ACT.Exp,
                        bias=d_min[n, part][:, j : j + 1],
                        scale=-1.0,
                        accum_out=weight_sums[n, part][:, j : j + 1],
                    )

        def invert_sums(n):
            for part in parts_of(n):
                inverse_sums[n, part] = work.tile([P, part_tiles(n)], F32, name="inverse_sums", tag="inverse_sums")
                nc.vector.reciprocal(out=inverse_sums[n, part][:], in_=weight_sums[n, part][:])

        def return_att(n):
            for part in parts_of(n):
                att = work.tile([P, part_tiles(n), C], F32, name="att", tag="att", bufs=LONG)
                for j in range(part_tiles(n)):
                    nc.vector.tensor_scalar_mul(
                        out=att[:, j, :], in0=weights[n, part][:, j, :], scalar1=inverse_sums[n, part][:, j : j + 1]
                    )
                columns = slice(part * part_tiles(n) * C, (part + 1) * part_tiles(n) * C)
                nc.sync.dma_start(out=att_chunks[n][:, columns], in_=att[:].rearrange("p j c -> p (j c)"))

        for half in range(2):
            flip_x(0, half)
            group_x(0, half)
        quantise_x(0)

        w_ls_codes = const.tile([P, H], U32, name="w_ls_codes", align_bytes=64)
        w_ls_scales = const.tile([P, H], U8, name="w_ls_scales", align_bytes=64)
        w_mu_codes = const.tile([P, H], U32, name="w_mu_codes", align_bytes=64)
        w_mu_scales = const.tile([P, H], U8, name="w_mu_scales", align_bytes=64)
        for rows, codes, scales in ((w_ls_rows, w_ls_codes, w_ls_scales), (w_mu_rows, w_mu_codes, w_mu_scales)):
            w_grouped = new_grouped(H)
            group_words(flip_words(rows, 0), w_grouped, 0, scalar_copy)
            group_words(flip_words(rows, 1), w_grouped, 1, scalar_copy)
            quantise(w_grouped[:], codes, scales)

        bias_cols = bank([P, P], BF16)
        nc.tensor.transpose(bias_cols[:], bias_rows[:], ident_bf16[:])
        b_mu_cols = const.tile([P, H_TILES], F32, name="b_mu_cols")
        nc.vector.tensor_copy(out=b_mu_cols[:], in_=bias_cols[:, 0:H_TILES])
        half_b_ls_cols = const.tile([P, H_TILES], F32, name="half_b_ls_cols")
        nc.vector.tensor_scalar_mul(out=half_b_ls_cols[:], in0=bias_cols[:, H_TILES : 2 * H_TILES], scalar1=0.5)

        cluster_grouped = const.tile([P, 2, C, PACK], BF16, name="cluster_grouped", align_bytes=64)
        for operand, (rows, factor) in enumerate(((inv_sig, 1.0), (mu_inv, -2.0))):
            flipped = bank([P, H_TILES, C], F32)
            for t in range(H_TILES):
                nc.tensor.transpose(flipped[:, t, :], rows[:, t * P : (t + 1) * P], ident_f32[:])
            nc.scalar.mul(
                out=cluster_grouped[:, operand], in_=flipped[:].rearrange("p t c -> p c t"), mul=factor
            )
        cluster_codes = const.tile([P, 2 * C], U32, name="cluster_codes", align_bytes=64)
        cluster_scales = const.tile([P, 2 * C], U8, name="cluster_scales", align_bytes=64)
        quantise(cluster_grouped[:].rearrange("p o c t -> p (o c t)"), cluster_codes, cluster_scales)
        c2_flipped = bank([P, C], F32)
        nc.tensor.transpose(c2_flipped[:], c2_repeated[:], ident_f32[:])
        c2_rows = const.tile([P, C], F32, name="c2_rows")
        nc.vector.tensor_copy(out=c2_rows[:], in_=c2_flipped[:])

        for step in range(-FILL_STEPS, N_STEPS + DRAIN_STEPS):
            n, t = divmod(step, H_TILES)
            if t == 0 and n >= 0:
                quantise_x(n + 1)
            if t == 2:
                quantise_z(n - 1)
            sigma_of(step + 3)
            if t % 2 == 1:
                noise_of(step + 1)
            z_of(step)
            if t == 0:
                group_z(n - 1)
                group_zz(n - 1)
                return_z(n - 1, 0)
            if t == 1:
                return_z(n - 1, 1)
                row_minimum(n - 2)
            if t == 2:
                return_z(n - 1, 2)
                group_x(n + 2, 0)
                exponentials(n - 2)
                return_att(n - 3)
            if t == 3:
                return_z(n - 1, 3)
                group_x(n + 2, 1)
                add_c2(n - 1)
                invert_sums(n - 2)

            mu_product(step + 1)
            ls_product(step + 4)
            if t == 0:
                flip_eps(n, 3)
                flip_z_back(n - 1, 1)
            if t == 1:
                flip_eps(n + 1, 0)
                flip_z_back(n - 1, 2)
                flip_x(n + 2, 0)
            if t == 2:
                flip_eps(n + 1, 1)
                flip_z_back(n - 1, 3)
                flip_x(n + 2, 1)
                second_products(n - 1)
            if t == 3:
                flip_eps(n + 1, 2)
                flip_z_back(n, 0)
